import numpy as np
import ml_dtypes


def mxq(x, axis, fmt="e4m3"):
    dtype, down = {"e4m3": (ml_dtypes.float8_e4m3fn, 7), "e5m2": (ml_dtypes.float8_e5m2, 14)}[fmt]
    v = np.moveaxis(np.asarray(x, np.float32).astype(ml_dtypes.bfloat16).astype(np.float64), axis, -1)
    blocks = v.reshape(v.shape[:-1] + (-1, 32))
    amax = np.abs(blocks).max(-1, keepdims=True)
    byte = np.maximum(np.where(amax > 0, np.frexp(amax)[1] - 1 + 127, 0) - down, 1)
    scale = np.exp2(byte - 127.0)
    codes = (blocks / scale).astype(np.float32).astype(dtype).astype(np.float64)
    return np.moveaxis((codes * scale).reshape(v.shape), -1, axis)


WIDE = False


def mx_kscale(k):
    if not WIDE:
        return np.ones(k)
    levels = np.array([10, -10, 5, -5, 0])
    if k % 512:
        return np.exp2(np.random.permutation(np.resize(levels, k // 32))).repeat(32)
    a = np.empty((k // 512, 16))
    for p in range(k // 512):
        a[p, :8] = np.random.permutation(np.resize(levels, 8))
        for g in range(8):
            far = levels[np.abs(levels - a[p, g]) >= 10]
            a[p, g + 8] = far[np.random.randint(len(far))]
    return np.exp2(a.ravel()).repeat(32)


BF16 = ml_dtypes.bfloat16


def bf(x):
    return np.asarray(x, np.float32).astype(BF16)


def f64(x):
    return np.asarray(x).astype(np.float64)


B, N, D, E, M, R = 1, 1024, 1024, 1024, 4096, 4
EPS = 1e-6


def layer_norm(v, g, b):
    mu = v.mean(-1, keepdims=True)
    var = ((v - mu) ** 2).mean(-1, keepdims=True)
    return (v - mu) / np.sqrt(var + EPS) * g + b


def merge(t):
    return t.reshape(B, N // R, R, E).mean(axis=2)


def setup_inputs():
    s = mx_kscale(D)

    def w():
        return bf(np.random.standard_normal((E, D)) * 2.0 / np.sqrt(D) / s)

    def c():
        return bf(np.random.standard_normal(E) * 0.3)

    x = np.random.standard_normal((B, N, D)) * (0.5 + 1.5 * np.random.random((B, N, 1))) + np.random.standard_normal((B, N, 1))
    return {"x": bf(x),
            "ln1_g": bf((1.0 + 0.1 * np.random.standard_normal(D)) * s),
            "ln1_b": bf(0.1 * np.random.standard_normal(D) * s),
            "Wq": w(), "bq": c(), "Wk": w(), "bk": c(), "Wv": w(), "bv": c()}


def reference(x, ln1_g, ln1_b, Wq, bq, Wk, bk, Wv, bv):
    h = layer_norm(f64(x), f64(ln1_g), f64(ln1_b))
    hq = mxq(h, 2, "e4m3")
    Q = (hq @ mxq(f64(Wq), 1, "e4m3").T) + f64(bq)
    K = (hq @ mxq(f64(Wk), 1, "e4m3").T) + f64(bk)
    V = (hq @ mxq(f64(Wv), 1, "e4m3").T) + f64(bv)
    return Q, merge(K), merge(V)

@@ -1,0 +1,322 @@
+from contextlib import ExitStack
+
+import concourse.mybir as mybir
+from concourse.masks import make_identity
+
+F32 = mybir.dt.float32
+BF16 = mybir.dt.bfloat16
+U32 = mybir.dt.uint32
+U8 = mybir.dt.uint8
+FP8X4 = mybir.dt.float8_e4m3fn_x4
+ACT = mybir.ActivationFunctionType
+ALU = mybir.AluOpType
+
+P = 128
+TOKENS = 1024
+D = 1024
+E = 1024
+MERGE = 4
+EPS = 1e-6
+PACK = 4
+K_PASS = P * PACK
+PASSES = D // K_PASS
+CHUNKS = D // P
+HALF = P * MERGE
+HALVES = TOKENS // HALF
+N_TILE = 512
+N_TILES = E // N_TILE
+RUN = N_TILE // P
+BN_MAX = 512
+
+FLOPS = 2 * 3 * TOKENS * D * E
+
+
+def tile_siglipencoderlayer_pa_kernel(
+    tc, x, ln1_g, ln1_b, Wq, bq, Wk, bk, Wv, bv, out_0, out_1, out_2
+):
+    nc = tc.nc
+    x_view = x.flatten_outer_dims().rearrange("(h j r) d -> j h r d", h=HALVES, r=MERGE)
+    q_view = out_0.flatten_outer_dims().rearrange("(h j r) e -> j h r e", h=HALVES, r=MERGE)
+    merged_views = {
+        "k": out_1.flatten_outer_dims().rearrange("(h j) e -> j h e", h=HALVES),
+        "v": out_2.flatten_outer_dims().rearrange("(h j) e -> j h e", h=HALVES),
+    }
+    weights = {"q": Wq, "k": Wk, "v": Wv}
+    biases = {"q": bq, "k": bk, "v": bv}
+
+    with ExitStack() as stack:
+        consts = stack.enter_context(tc.tile_pool(name="consts", bufs=1))
+        raw = stack.enter_context(tc.tile_pool(name="raw", bufs=1))
+        small = stack.enter_context(tc.tile_pool(name="small", bufs=2))
+        normed = stack.enter_context(tc.tile_pool(name="normed", bufs=2 * MERGE))
+        grouped = stack.enter_context(tc.tile_pool(name="grouped", bufs=3))
+        packed = stack.enter_context(tc.tile_pool(name="packed", bufs=1))
+        results = stack.enter_context(tc.tile_pool(name="results", bufs=6))
+        banks = stack.enter_context(tc.psum_pool(name="banks", bufs=8))
+        stack.enter_context(tc.manual_schedule())
+
+        ident = consts.tile([P, P], F32, name="ident")
+        make_identity(nc, ident[:])
+        eps = consts.tile([P, 1], F32, name="eps")
+        nc.vector.memset(eps[:], EPS)
+        warm = consts.tile([P, 1], F32, name="warm")
+        nc.scalar.activation(out=warm[:], in_=eps[:], func=ACT.Sqrt)
+
+        gb_rows = consts.tile([P, K_PASS], BF16, name="gb_rows")
+        nc.vector.memset(gb_rows[:], 0.0)
+        nc.scalar.dma_start(out=gb_rows[0:PASSES, :], in_=ln1_g.rearrange("(c w) -> c w", c=PASSES))
+        nc.scalar.dma_start(out=gb_rows[PASSES : 2 * PASSES, :], in_=ln1_b.rearrange("(c w) -> c w", c=PASSES))
+
+        x_raw = [raw.tile([P, MERGE, D], BF16, name="x_raw%d" % h) for h in range(HALVES)]
+        w_raw = {n: raw.tile([P, N_TILES, RUN * D], BF16, name="w_raw_" + n) for n in "qkv"}
+        bias_all = {n: consts.tile([P, E], BF16, name="bias_all_" + n) for n in "qkv"}
+
+        def load_weight(n, nt, i):
+            rows = weights[n].rearrange("(nt i p) d -> p nt i d", nt=N_TILES, p=P)
+            nc.sync.dma_start(out=w_raw[n][:, nt, i * D : (i + 1) * D], in_=rows[:, nt, i, :])
+
+        def load_bias(n):
+            nc.sync.dma_start(out=bias_all[n][:], in_=biases[n].partition_broadcast(P))
+
+        for i in range(RUN):
+            nc.sync.dma_start(out=x_raw[0][:, i, :], in_=x_view[:, 0, i, :])
+            load_weight("q", 0, i)
+        nc.sync.dma_start(out=x_raw[1][:], in_=x_view[:, 1, :, :])
+        for i in range(RUN):
+            load_weight("q", 1, i)
+        load_bias("q")
+        for n in "kv":
+            for nt in range(N_TILES):
+                for i in range(RUN):
+                    load_weight(n, nt, i)
+            load_bias(n)
+
+        gain_bias = consts.tile([P, 2 * CHUNKS], F32, name="gain_bias")
+        h_planes = packed.tile([P, CHUNKS, TOKENS], BF16, name="h_planes")
+        h_words = packed.tile([P, PASSES, TOKENS], U32, name="h_words", align_bytes=64)
+        h_scales = packed.tile([P, PASSES, TOKENS], U8, name="h_scales", align_bytes=64)
+        w_words = {
+            n: packed.tile([P, N_TILES, PASSES * N_TILE], U32, name="w_words_" + n, align_bytes=64)
+            for n in "qkv"
+        }
+        w_scales = {
+            n: packed.tile([P, N_TILES, PASSES * N_TILE], U8, name="w_scales_" + n, align_bytes=64)
+            for n in "qkv"
+        }
+        w_grouped = {}
+        xn_tiles = {}
+        moments = {}
+        mean_vars = {}
+
+        def flip_gain_bias():
+            bank = banks.tile([P, N_TILE], F32, tag="bank")
+            words = gb_rows[:].bitcast(F32).rearrange("p (q u) -> p u q", u=2)
+            for u in range(2):
+                nc.tensor.transpose(out=bank[:, u * P : (u + 1) * P], in_=words[:, u, :], identity=ident[:])
+            src = bank[:].bitcast(BF16)[:, 0 : 4 * P].rearrange("p (u c e) -> p c u e", u=2, e=2)
+            nc.vector.tensor_copy(
+                out=gain_bias[:].rearrange("p (c u e) -> p c u e", u=2, e=2), in_=src[:, 0 : 2 * PASSES, :, :]
+            )
+
+        def flip_weight_bank(n, nt, i, engine):
+            if i == 0:
+                w_grouped[(n, nt)] = grouped.tile(
+                    [P, PASSES * N_TILE * PACK], BF16, name="w_grouped", tag="w_grouped", align_bytes=64
+                )
+            words_in = w_raw[n][:, nt, :].bitcast(F32).rearrange(
+                "p (i g q u) -> p i g u q", i=RUN, g=PASSES, u=2
+            )
+            words_out = w_grouped[(n, nt)][:].bitcast(F32).rearrange(
+                "p (g e u) -> p g e u", g=PASSES, u=2
+            )
+            bank = banks.tile([P, N_TILE], F32, tag="bank")
+            for c in range(PASSES * 2):
+                nc.tensor.transpose(
+                    out=bank[:, c * P : (c + 1) * P], in_=words_in[:, i, c // 2, c % 2, :], identity=ident[:]
+                )
+            dst = words_out[:, :, i * P : (i + 1) * P, :]
+            src = bank[:].rearrange("p (g u e) -> p g e u", g=PASSES, u=2)
+            if engine == "vector":
+                nc.vector.tensor_copy(out=dst, in_=src)
+            else:
+                nc.scalar.copy(out=dst, in_=src)
+
+        def flip_weight(n, nt, vector_banks):
+            for i in range(RUN):
+                flip_weight_bank(n, nt, i, "vector" if i < vector_banks else "scalar")
+
+        def pack_weight(n, nt):
+            nc.vector.quantize_mx(
+                out=w_words[n][:, nt, :].bitcast(FP8X4),
+                scales=w_scales[n][:, nt, :],
+                in_=w_grouped[(n, nt)][:],
+            )
+
+        def measure_tile(h, r):
+            if r == 0:
+                mean_vars[h] = small.tile([P, MERGE, 2], F32, name="mean_var", tag="mean_var")
+            stats = small.tile([P, D // BN_MAX, 6], F32, tag="stats")
+            for s in range(D // BN_MAX):
+                nc.vector.bn_stats(
+                    out=stats[:, s, :], in_=x_raw[h][:, r, s * BN_MAX : (s + 1) * BN_MAX]
+                )
+            nc.vector.bn_aggr(out=mean_vars[h][:, r, :], in_=stats[:].rearrange("p s k -> p (s k)"))
+
+        def finish_measure(h):
+            mean_var = mean_vars[h]
+            std = small.tile([P, MERGE], F32, tag="std")
+            nc.scalar.activation(out=std[:], in_=mean_var[:, :, 1], func=ACT.Sqrt, bias=eps[:, 0:1])
+            rstd = small.tile([P, MERGE], F32, tag="rstd")
+            nc.vector.reciprocal(out=rstd[:], in_=std[:])
+            shift = small.tile([P, MERGE], F32, tag="shift")
+            nc.vector.scalar_tensor_tensor(
+                out=shift[:], in0=mean_var[:, :, 0], scalar=-1.0, in1=rstd[:], op0=ALU.mult, op1=ALU.mult
+            )
+            moments[h] = (rstd, shift)
+
+        def normalise(h, r, engine):
+            rstd, shift = moments[h]
+            xn = normed.tile([P, D], F32, tag="xn")
+            xn_tiles[(h, r)] = xn
+            dst = xn[:].rearrange("p (g t q) -> p g t q", g=PASSES, t=PACK)
+            src = x_raw[h][:, r, :].rearrange("p (g q t) -> p g t q", g=PASSES, t=PACK)
+            if engine == "scalar":
+                nc.scalar.activation(
+                    out=dst, in_=src, func=ACT.Identity, scale=rstd[:, r : r + 1], bias=shift[:, r : r + 1]
+                )
+            elif engine == "vector":
+                nc.vector.tensor_scalar(
+                    out=dst, in0=src, scalar1=rstd[:, r : r + 1], scalar2=shift[:, r : r + 1],
+                    op0=ALU.mult, op1=ALU.add,
+                )
+            else:
+                nc.gpsimd.tensor_scalar(
+                    out=dst, in0=src, scalar1=rstd[:, r : r + 1], scalar2=shift[:, r : r + 1],
+                    op0=ALU.mult, op1=ALU.add,
+                )
+
+        def flip_tokens(h, g, vector_banks):
+            toks = slice(h * HALF, (h + 1) * HALF)
+            for t in range(PACK):
+                f = g * PACK + t
+                bank = banks.tile([P, N_TILE], F32, tag="bank")
+                for r in range(MERGE):
+                    nc.tensor.transpose(
+                        out=bank[:, r * P : (r + 1) * P],
+                        in_=xn_tiles[(h, r)][:, f * P : (f + 1) * P],
+                        identity=ident[:],
+                    )
+                gain = gain_bias[:, f : f + 1]
+                bias = gain_bias[:, CHUNKS + f : CHUNKS + f + 1]
+                if t < vector_banks:
+                    nc.vector.tensor_scalar(
+                        out=h_planes[:, f, toks], in0=bank[:], scalar1=gain, scalar2=bias,
+                        op0=ALU.mult, op1=ALU.add,
+                    )
+                else:
+                    nc.scalar.activation(
+                        out=h_planes[:, f, toks], in_=bank[:], func=ACT.Identity, scale=gain, bias=bias
+                    )
+
+        h_grouped = {}
+
+        def group_tokens(h, g, engine):
+            toks = slice(h * HALF, (h + 1) * HALF)
+            tile_ = grouped.tile([P, HALF * PACK], BF16, tag="h_grouped", align_bytes=64)
+            h_grouped[(h, g)] = tile_
+            dst = tile_[:].rearrange("p (n t) -> p n t", t=PACK)
+            src = h_planes[:, g * PACK : (g + 1) * PACK, toks].rearrange("p t n -> p n t")
+            if engine == "vector":
+                nc.vector.tensor_copy(out=dst, in_=src)
+            else:
+                nc.scalar.copy(out=dst, in_=src)
+
+        def pack_tokens(h, g):
+            toks = slice(h * HALF, (h + 1) * HALF)
+            nc.vector.quantize_mx(
+                out=h_words[:, g, toks].bitcast(FP8X4), scales=h_scales[:, g, toks],
+                in_=h_grouped[(h, g)][:],
+            )
+
+        def one_pass(acc, n, h, r, g, nt, start, stop):
+            toks = slice(h * HALF + r * P, h * HALF + (r + 1) * P)
+            cols = slice(g * N_TILE, (g + 1) * N_TILE)
+            nc.tensor.matmul_mx(
+                out=acc[:],
+                lhsT=h_words[:, g, toks].bitcast(FP8X4),
+                lhsT_scale=h_scales[:, g, toks],
+                rhs=w_words[n][:, nt, cols].bitcast(FP8X4),
+                rhs_scale=w_scales[n][:, nt, cols],
+                start=start,
+                stop=stop,
+            )
+
+        def queries(h, nt):
+            cols = slice(nt * N_TILE, (nt + 1) * N_TILE)
+            for r in range(MERGE):
+                acc = banks.tile([P, N_TILE], F32, tag="bank")
+                for g in range(PASSES):
+                    one_pass(acc, "q", h, r, g, nt, g == 0, g == PASSES - 1)
+                rows = results.tile([P, N_TILE], F32, tag="rows")
+                nc.vector.tensor_tensor(out=rows[:], in0=acc[:], in1=bias_all["q"][:, cols], op=ALU.add)
+                nc.sync.dma_start(out=q_view[:, h, r, cols], in_=rows[:])
+
+        def merged(n, h, nt):
+            cols = slice(nt * N_TILE, (nt + 1) * N_TILE)
+            acc = banks.tile([P, N_TILE], F32, tag="bank")
+            for r in range(MERGE):
+                for g in range(PASSES):
+                    one_pass(acc, n, h, r, g, nt, r == 0 and g == 0, r == MERGE - 1 and g == PASSES - 1)
+            rows = results.tile([P, N_TILE], F32, tag="rows")
+            nc.vector.scalar_tensor_tensor(
+                out=rows[:], in0=acc[:], scalar=1.0 / MERGE, in1=bias_all[n][:, cols],
+                op0=ALU.mult, op1=ALU.add,
+            )
+            nc.sync.dma_start(out=merged_views[n][:, h, cols], in_=rows[:])
+
+        for i in range(RUN):
+            measure_tile(0, i)
+            flip_weight_bank("q", 0, i, "scalar")
+        finish_measure(0)
+        flip_gain_bias()
+        for r in range(MERGE):
+            normalise(0, r, "gpsimd" if r % 2 == 0 else "scalar")
+        for r in range(MERGE):
+            measure_tile(1, r)
+        flip_tokens(0, 0, 0)
+        flip_tokens(0, 1, 0)
+        pack_weight("q", 0)
+        group_tokens(0, 0, "vector")
+        pack_tokens(0, 0)
+        group_tokens(0, 1, "vector")
+        pack_tokens(0, 1)
+        finish_measure(1)
+        flip_weight("q", 1, 0)
+        for r in range(MERGE):
+            normalise(1, r, "gpsimd" if r % 2 == 0 else "scalar")
+        queries(0, 0)
+        pack_weight("q", 1)
+        flip_tokens(1, 0, 0)
+        flip_tokens(1, 1, 0)
+        queries(0, 1)
+        group_tokens(1, 0, "vector")
+        pack_tokens(1, 0)
+        flip_weight("k", 0, 0)
+        group_tokens(1, 1, "vector")
+        pack_tokens(1, 1)
+        flip_weight("k", 1, 0)
+        queries(1, 0)
+        pack_weight("k", 0)
+        queries(1, 1)
+        pack_weight("k", 1)
+        flip_weight("v", 0, 0)
+        merged("k", 0, 0)
+        merged("k", 1, 0)
+        flip_weight("v", 1, 0)
+        pack_weight("v", 0)
+        merged("k", 0, 1)
+        merged("k", 1, 1)
+        pack_weight("v", 1)
+        for nt in range(N_TILES):
+            for h in range(HALVES):
+                merged("v", h, nt)

@@ -23,6 +23,10 @@ PASSES = D // K_PASS
 CHUNKS = D // P
 HALF = P * MERGE
 HALVES = TOKENS // HALF
+TILES = TOKENS // P
+PAIR = 2
+UNITS = TILES // PAIR
+UNIT = PAIR * P
 N_TILE = 512
 N_TILES = E // N_TILE
 RUN = N_TILE // P
@@ -47,11 +51,12 @@ def tile_siglipencoderlayer_pa_kernel(
     with ExitStack() as stack:
         consts = stack.enter_context(tc.tile_pool(name="consts", bufs=1))
         raw = stack.enter_context(tc.tile_pool(name="raw", bufs=1))
-        small = stack.enter_context(tc.tile_pool(name="small", bufs=2))
-        normed = stack.enter_context(tc.tile_pool(name="normed", bufs=2 * MERGE))
-        grouped = stack.enter_context(tc.tile_pool(name="grouped", bufs=3))
+        small = stack.enter_context(tc.tile_pool(name="small", bufs=4))
+        normed = stack.enter_context(tc.tile_pool(name="normed", bufs=TILES))
+        planes = stack.enter_context(tc.tile_pool(name="planes", bufs=2))
+        grouped = stack.enter_context(tc.tile_pool(name="grouped", bufs=4))
         packed = stack.enter_context(tc.tile_pool(name="packed", bufs=1))
-        results = stack.enter_context(tc.tile_pool(name="results", bufs=6))
+        results = stack.enter_context(tc.tile_pool(name="results", bufs=10))
         banks = stack.enter_context(tc.psum_pool(name="banks", bufs=8))
         stack.enter_context(tc.manual_schedule())
 
@@ -60,14 +65,14 @@ def tile_siglipencoderlayer_pa_kernel(
         eps = consts.tile([P, 1], F32, name="eps")
         nc.vector.memset(eps[:], EPS)
         warm = consts.tile([P, 1], F32, name="warm")
-        nc.scalar.activation(out=warm[:], in_=eps[:], func=ACT.Sqrt)
+        nc.scalar.activation(out=warm[:], in_=eps[:], func=ACT.Abs_reciprocal_sqrt)
 
         gb_rows = consts.tile([P, K_PASS], BF16, name="gb_rows")
         nc.vector.memset(gb_rows[:], 0.0)
         nc.scalar.dma_start(out=gb_rows[0:PASSES, :], in_=ln1_g.rearrange("(c w) -> c w", c=PASSES))
         nc.scalar.dma_start(out=gb_rows[PASSES : 2 * PASSES, :], in_=ln1_b.rearrange("(c w) -> c w", c=PASSES))
 
-        x_raw = [raw.tile([P, MERGE, D], BF16, name="x_raw%d" % h) for h in range(HALVES)]
+        x_raw = [raw.tile([P, D], BF16, name="x_raw%d" % i) for i in range(TILES)]
         w_raw = {n: raw.tile([P, N_TILES, RUN * D], BF16, name="w_raw_" + n) for n in "qkv"}
         bias_all = {n: consts.tile([P, E], BF16, name="bias_all_" + n) for n in "qkv"}
 
@@ -78,23 +83,20 @@ def tile_siglipencoderlayer_pa_kernel(
         def load_bias(n):
             nc.sync.dma_start(out=bias_all[n][:], in_=biases[n].partition_broadcast(P))
 
-        for i in range(RUN):
-            nc.sync.dma_start(out=x_raw[0][:, i, :], in_=x_view[:, 0, i, :])
-            load_weight("q", 0, i)
-        nc.sync.dma_start(out=x_raw[1][:], in_=x_view[:, 1, :, :])
-        for i in range(RUN):
-            load_weight("q", 1, i)
-        load_bias("q")
-        for n in "kv":
-            for nt in range(N_TILES):
-                for i in range(RUN):
-                    load_weight(n, nt, i)
+        blocks = [(n, nt, i) for n in "kvq" for nt in range(N_TILES) for i in range(RUN)]
+        for i in range(TILES):
+            nc.sync.dma_start(out=x_raw[i][:], in_=x_view[:, i // MERGE, i % MERGE, :])
+            if i % PAIR == PAIR - 1:
+                for c in range(i - 1, i + 1):
+                    load_weight(*blocks[c])
+        for c in range(TILES, len(blocks)):
+            load_weight(*blocks[c])
+        for n in "kvq":
             load_bias(n)
 
         gain_bias = consts.tile([P, 2 * CHUNKS], F32, name="gain_bias")
-        h_planes = packed.tile([P, CHUNKS, TOKENS], BF16, name="h_planes")
-        h_words = packed.tile([P, PASSES, TOKENS], U32, name="h_words", align_bytes=64)
-        h_scales = packed.tile([P, PASSES, TOKENS], U8, name="h_scales", align_bytes=64)
+        h_words = packed.tile([P, UNITS, PASSES * UNIT], U32, name="h_words", align_bytes=64)
+        h_scales = packed.tile([P, UNITS, PASSES * UNIT], U8, name="h_scales", align_bytes=64)
         w_words = {
             n: packed.tile([P, N_TILES, PASSES * N_TILE], U32, name="w_words_" + n, align_bytes=64)
             for n in "qkv"
@@ -105,7 +107,7 @@ def tile_siglipencoderlayer_pa_kernel(
         }
         w_grouped = {}
         xn_tiles = {}
-        moments = {}
+        rstds = {}
         mean_vars = {}
 
         def flip_gain_bias():
@@ -118,7 +120,7 @@ def tile_siglipencoderlayer_pa_kernel(
                 out=gain_bias[:].rearrange("p (c u e) -> p c u e", u=2, e=2), in_=src[:, 0 : 2 * PASSES, :, :]
             )
 
-        def flip_weight_bank(n, nt, i, engine):
+        def flip_weight(n, nt, i, engine="scalar"):
             if i == 0:
                 w_grouped[(n, nt)] = grouped.tile(
                     [P, PASSES * N_TILE * PACK], BF16, name="w_grouped", tag="w_grouped", align_bytes=64
@@ -141,10 +143,6 @@ def tile_siglipencoderlayer_pa_kernel(
             else:
                 nc.scalar.copy(out=dst, in_=src)
 
-        def flip_weight(n, nt, vector_banks):
-            for i in range(RUN):
-                flip_weight_bank(n, nt, i, "vector" if i < vector_banks else "scalar")
-
         def pack_weight(n, nt):
             nc.vector.quantize_mx(
                 out=w_words[n][:, nt, :].bitcast(FP8X4),
@@ -152,171 +150,223 @@ def tile_siglipencoderlayer_pa_kernel(
                 in_=w_grouped[(n, nt)][:],
             )
 
-        def measure_tile(h, r):
-            if r == 0:
-                mean_vars[h] = small.tile([P, MERGE, 2], F32, name="mean_var", tag="mean_var")
+        stats_tiles = {}
+
+        def measure_tile(i):
             stats = small.tile([P, D // BN_MAX, 6], F32, tag="stats")
+            stats_tiles[i] = stats
             for s in range(D // BN_MAX):
-                nc.vector.bn_stats(
-                    out=stats[:, s, :], in_=x_raw[h][:, r, s * BN_MAX : (s + 1) * BN_MAX]
-                )
-            nc.vector.bn_aggr(out=mean_vars[h][:, r, :], in_=stats[:].rearrange("p s k -> p (s k)"))
+                nc.vector.bn_stats(out=stats[:, s, :], in_=x_raw[i][:, s * BN_MAX : (s + 1) * BN_MAX])
 
-        def finish_measure(h):
-            mean_var = mean_vars[h]
-            std = small.tile([P, MERGE], F32, tag="std")
-            nc.scalar.activation(out=std[:], in_=mean_var[:, :, 1], func=ACT.Sqrt, bias=eps[:, 0:1])
-            rstd = small.tile([P, MERGE], F32, tag="rstd")
-            nc.vector.reciprocal(out=rstd[:], in_=std[:])
-            shift = small.tile([P, MERGE], F32, tag="shift")
-            nc.vector.scalar_tensor_tensor(
-                out=shift[:], in0=mean_var[:, :, 0], scalar=-1.0, in1=rstd[:], op0=ALU.mult, op1=ALU.mult
+        def join_moments(i):
+            u = i // PAIR
+            if i % PAIR == 0:
+                mean_vars[u] = small.tile([P, PAIR, 2], F32, name="mean_var", tag="mean_var")
+            nc.vector.bn_aggr(
+                out=mean_vars[u][:, i % PAIR, :], in_=stats_tiles[i][:].rearrange("p s k -> p (s k)")
             )
-            moments[h] = (rstd, shift)
 
-        def normalise(h, r, engine):
-            rstd, shift = moments[h]
+        def finish_measure(u):
+            mean_var = mean_vars[u]
+            rstd = small.tile([P, PAIR], F32, tag="rstd")
+            nc.scalar.activation(
+                out=rstd[:], in_=mean_var[:, :, 1], func=ACT.Abs_reciprocal_sqrt, bias=eps[:, 0:1]
+            )
+            rstds[u] = rstd
+
+
+        def normalise(i, engine="vector"):
+            u, r = i // PAIR, i % PAIR
+            rstd = rstds[u]
             xn = normed.tile([P, D], F32, tag="xn")
-            xn_tiles[(h, r)] = xn
+            xn_tiles[i] = xn
             dst = xn[:].rearrange("p (g t q) -> p g t q", g=PASSES, t=PACK)
-            src = x_raw[h][:, r, :].rearrange("p (g q t) -> p g t q", g=PASSES, t=PACK)
-            if engine == "scalar":
-                nc.scalar.activation(
-                    out=dst, in_=src, func=ACT.Identity, scale=rstd[:, r : r + 1], bias=shift[:, r : r + 1]
-                )
-            elif engine == "vector":
-                nc.vector.tensor_scalar(
-                    out=dst, in0=src, scalar1=rstd[:, r : r + 1], scalar2=shift[:, r : r + 1],
-                    op0=ALU.mult, op1=ALU.add,
-                )
-            else:
-                nc.gpsimd.tensor_scalar(
-                    out=dst, in0=src, scalar1=rstd[:, r : r + 1], scalar2=shift[:, r : r + 1],
-                    op0=ALU.mult, op1=ALU.add,
+            src = x_raw[i][:].rearrange("p (g q t) -> p g t q", g=PASSES, t=PACK)
+            if True:
+                eng = nc.vector if engine == "vector" else nc.gpsimd
+                eng.tensor_scalar(
+                    out=dst, in0=src, scalar1=mean_vars[u][:, r, 0:1], scalar2=rstd[:, r : r + 1],
+                    op0=ALU.subtract, op1=ALU.mult,
                 )
 
-        def flip_tokens(h, g, vector_banks):
-            toks = slice(h * HALF, (h + 1) * HALF)
-            for t in range(PACK):
-                f = g * PACK + t
+        h_plane = {}
+
+        def flip_tokens(u, g, vector_banks=0):
+            if g == 0:
+                h_plane[u] = planes.tile([P, CHUNKS, UNIT], BF16, name="h_plane", tag="h_plane")
+            for b in range(PACK // PAIR):
                 bank = banks.tile([P, N_TILE], F32, tag="bank")
-                for r in range(MERGE):
-                    nc.tensor.transpose(
-                        out=bank[:, r * P : (r + 1) * P],
-                        in_=xn_tiles[(h, r)][:, f * P : (f + 1) * P],
-                        identity=ident[:],
-                    )
-                gain = gain_bias[:, f : f + 1]
-                bias = gain_bias[:, CHUNKS + f : CHUNKS + f + 1]
-                if t < vector_banks:
-                    nc.vector.tensor_scalar(
-                        out=h_planes[:, f, toks], in0=bank[:], scalar1=gain, scalar2=bias,
-                        op0=ALU.mult, op1=ALU.add,
-                    )
-                else:
-                    nc.scalar.activation(
-                        out=h_planes[:, f, toks], in_=bank[:], func=ACT.Identity, scale=gain, bias=bias
-                    )
+                for s in range(PAIR):
+                    f = g * PACK + b * PAIR + s
+                    for r in range(PAIR):
+                        nc.tensor.transpose(
+                            out=bank[:, s * UNIT + r * P : s * UNIT + (r + 1) * P],
+                            in_=xn_tiles[u * PAIR + r][:, f * P : (f + 1) * P],
+                            identity=ident[:],
+                        )
+                for s in range(PAIR):
+                    f = g * PACK + b * PAIR + s
+                    gain = gain_bias[:, f : f + 1]
+                    bias = gain_bias[:, CHUNKS + f : CHUNKS + f + 1]
+                    src = bank[:, s * UNIT : (s + 1) * UNIT]
+                    if b < vector_banks:
+                        nc.vector.tensor_scalar(
+                            out=h_plane[u][:, f, :], in0=src, scalar1=gain, scalar2=bias,
+                            op0=ALU.mult, op1=ALU.add,
+                        )
+                    else:
+                        nc.scalar.activation(
+                            out=h_plane[u][:, f, :], in_=src, func=ACT.Identity, scale=gain, bias=bias
+                        )
 
         h_grouped = {}
 
-        def group_tokens(h, g, engine):
-            toks = slice(h * HALF, (h + 1) * HALF)
-            tile_ = grouped.tile([P, HALF * PACK], BF16, tag="h_grouped", align_bytes=64)
-            h_grouped[(h, g)] = tile_
-            dst = tile_[:].rearrange("p (n t) -> p n t", t=PACK)
-            src = h_planes[:, g * PACK : (g + 1) * PACK, toks].rearrange("p t n -> p n t")
+        def group_tokens(u, g, engine="vector"):
+            if g == 0:
+                h_grouped[u] = grouped.tile([P, PASSES, UNIT * PACK], BF16, name="h_grouped", tag="h_grouped", align_bytes=64)
+            dst = h_grouped[u][:, g, :].rearrange("p (n t) -> p n t", t=PACK)
+            src = h_plane[u][:, g * PACK : (g + 1) * PACK, :].rearrange("p t n -> p n t")
             if engine == "vector":
                 nc.vector.tensor_copy(out=dst, in_=src)
             else:
                 nc.scalar.copy(out=dst, in_=src)
 
-        def pack_tokens(h, g):
-            toks = slice(h * HALF, (h + 1) * HALF)
+        def pack_tokens(u):
             nc.vector.quantize_mx(
-                out=h_words[:, g, toks].bitcast(FP8X4), scales=h_scales[:, g, toks],
-                in_=h_grouped[(h, g)][:],
+                out=h_words[:, u, :].bitcast(FP8X4), scales=h_scales[:, u, :],
+                in_=h_grouped[u][:].rearrange("p g w -> p (g w)"),
             )
 
-        def one_pass(acc, n, h, r, g, nt, start, stop):
-            toks = slice(h * HALF + r * P, h * HALF + (r + 1) * P)
+        def one_pass(acc, n, i, g, nt, start, stop):
+            u = i // PAIR
+            toks = slice(g * UNIT + (i % PAIR) * P, g * UNIT + (i % PAIR) * P + P)
             cols = slice(g * N_TILE, (g + 1) * N_TILE)
             nc.tensor.matmul_mx(
                 out=acc[:],
-                lhsT=h_words[:, g, toks].bitcast(FP8X4),
-                lhsT_scale=h_scales[:, g, toks],
+                lhsT=h_words[:, u, toks].bitcast(FP8X4),
+                lhsT_scale=h_scales[:, u, toks],
                 rhs=w_words[n][:, nt, cols].bitcast(FP8X4),
                 rhs_scale=w_scales[n][:, nt, cols],
                 start=start,
                 stop=stop,
             )
 
-        def queries(h, nt):
-            cols = slice(nt * N_TILE, (nt + 1) * N_TILE)
-            for r in range(MERGE):
-                acc = banks.tile([P, N_TILE], F32, tag="bank")
-                for g in range(PASSES):
-                    one_pass(acc, "q", h, r, g, nt, g == 0, g == PASSES - 1)
-                rows = results.tile([P, N_TILE], F32, tag="rows")
-                nc.vector.tensor_tensor(out=rows[:], in0=acc[:], in1=bias_all["q"][:, cols], op=ALU.add)
-                nc.sync.dma_start(out=q_view[:, h, r, cols], in_=rows[:])
-
-        def merged(n, h, nt):
+        def queries(i, nt):
             cols = slice(nt * N_TILE, (nt + 1) * N_TILE)
             acc = banks.tile([P, N_TILE], F32, tag="bank")
-            for r in range(MERGE):
+            for g in range(PASSES):
+                one_pass(acc, "q", i, g, nt, g == 0, g == PASSES - 1)
+            rows = results.tile([P, N_TILE], F32, tag="rows")
+            nc.vector.tensor_tensor(out=rows[:], in0=acc[:], in1=bias_all["q"][:, cols], op=ALU.add)
+            nc.sync.dma_start(out=q_view[:, i // MERGE, i % MERGE, cols], in_=rows[:])
+
+        accs = {}
+
+        def merged(n, h, nt, part):
+            if part == 0:
+                accs[(n, h, nt)] = banks.tile([P, N_TILE], F32, name="acc", tag="bank")
+            acc = accs[(n, h, nt)]
+            for r in range(PAIR):
                 for g in range(PASSES):
-                    one_pass(acc, n, h, r, g, nt, r == 0 and g == 0, r == MERGE - 1 and g == PASSES - 1)
+                    one_pass(
+                        acc, n, h * MERGE + part * PAIR + r, g, nt,
+                        part == 0 and r == 0 and g == 0, part == 1 and r == PAIR - 1 and g == PASSES - 1,
+                    )
+
+        def settle(n, h, nt):
+            cols = slice(nt * N_TILE, (nt + 1) * N_TILE)
             rows = results.tile([P, N_TILE], F32, tag="rows")
             nc.vector.scalar_tensor_tensor(
-                out=rows[:], in0=acc[:], scalar=1.0 / MERGE, in1=bias_all[n][:, cols],
+                out=rows[:], in0=accs[(n, h, nt)][:], scalar=1.0 / MERGE, in1=bias_all[n][:, cols],
                 op0=ALU.mult, op1=ALU.add,
             )
             nc.sync.dma_start(out=merged_views[n][:, h, cols], in_=rows[:])
 
-        for i in range(RUN):
-            measure_tile(0, i)
-            flip_weight_bank("q", 0, i, "scalar")
-        finish_measure(0)
+
+        def weights_run(first, last, vector=()):
+            for c in range(first, last):
+                flip_weight(*blocks[c], engine="vector" if c in vector else "scalar")
+
+        def stats(u):
+            join_moments(2 * u)
+            join_moments(2 * u + 1)
+            finish_measure(u)
+
+        def tokens(u):
+            flip_tokens(u, 0)
+            flip_tokens(u, 1)
+
+        def pack(u):
+            group_tokens(u, 0)
+            group_tokens(u, 1)
+            pack_tokens(u)
+
+        measure_tile(0)
+        weights_run(0, 1)
+        measure_tile(1)
+        weights_run(1, 2)
+        stats(0)
+        measure_tile(2)
+        normalise(0)
+        normalise(1)
+        weights_run(2, 4)
         flip_gain_bias()
-        for r in range(MERGE):
-            normalise(0, r, "gpsimd" if r % 2 == 0 else "scalar")
-        for r in range(MERGE):
-            measure_tile(1, r)
-        flip_tokens(0, 0, 0)
-        flip_tokens(0, 1, 0)
-        pack_weight("q", 0)
-        group_tokens(0, 0, "vector")
-        pack_tokens(0, 0)
-        group_tokens(0, 1, "vector")
-        pack_tokens(0, 1)
-        finish_measure(1)
-        flip_weight("q", 1, 0)
-        for r in range(MERGE):
-            normalise(1, r, "gpsimd" if r % 2 == 0 else "scalar")
-        queries(0, 0)
-        pack_weight("q", 1)
-        flip_tokens(1, 0, 0)
-        flip_tokens(1, 1, 0)
-        queries(0, 1)
-        group_tokens(1, 0, "vector")
-        pack_tokens(1, 0)
-        flip_weight("k", 0, 0)
-        group_tokens(1, 1, "vector")
-        pack_tokens(1, 1)
-        flip_weight("k", 1, 0)
-        queries(1, 0)
+        measure_tile(3)
+        stats(1)
+        tokens(0)
+        measure_tile(4)
+        normalise(2)
+        normalise(3)
+        weights_run(4, 8)
+        measure_tile(5)
+        stats(2)
+        tokens(1)
+        pack(0)
         pack_weight("k", 0)
-        queries(1, 1)
+        measure_tile(6)
+        weights_run(8, 14)
+        normalise(4)
+        normalise(5)
+        measure_tile(7)
+        stats(3)
+        merged("k", 0, 0, 0)
+        weights_run(14, 18)
+        tokens(2)
+        pack(1)
         pack_weight("k", 1)
-        flip_weight("v", 0, 0)
-        merged("k", 0, 0)
-        merged("k", 1, 0)
-        flip_weight("v", 1, 0)
         pack_weight("v", 0)
-        merged("k", 0, 1)
-        merged("k", 1, 1)
+        normalise(6)
+        normalise(7)
+        weights_run(18, 21)
+        merged("k", 0, 1, 0)
+        weights_run(21, 24)
+        tokens(3)
         pack_weight("v", 1)
-        for nt in range(N_TILES):
-            for h in range(HALVES):
-                merged("v", h, nt)
+        merged("k", 0, 0, 1)
+        merged("k", 0, 1, 1)
+        pack(2)
+        merged("v", 0, 0, 0)
+        merged("v", 0, 0, 1)
+        settle("k", 0, 0)
+        pack_weight("q", 0)
+        merged("v", 0, 1, 0)
+        merged("v", 0, 1, 1)
+        settle("k", 0, 1)
+        pack(3)
+        merged("k", 1, 0, 0)
+        merged("k", 1, 1, 0)
+        settle("v", 0, 0)
+        pack_weight("q", 1)
+        settle("v", 0, 1)
+        merged("k", 1, 0, 1)
+        settle("k", 1, 0)
+        merged("k", 1, 1, 1)
+        settle("k", 1, 1)
+        for i in range(8):
+            queries(i, 0)
+            if i % 4 == 3:
+                merged("v", 1, i // 4, 0)
+                merged("v", 1, i // 4, 1)
+                settle("v", 1, i // 4)
+        for i in range(8):
+            queries(i, 1)

@@ -55,6 +55,7 @@ def tile_siglipencoderlayer_pa_kernel(
         normed = stack.enter_context(tc.tile_pool(name="normed", bufs=TILES))
         planes = stack.enter_context(tc.tile_pool(name="planes", bufs=2))
         grouped = stack.enter_context(tc.tile_pool(name="grouped", bufs=4))
+        sortp = stack.enter_context(tc.tile_pool(name="sortp", bufs=4))
         packed = stack.enter_context(tc.tile_pool(name="packed", bufs=1))
         results = stack.enter_context(tc.tile_pool(name="results", bufs=10))
         banks = stack.enter_context(tc.psum_pool(name="banks", bufs=8))
@@ -84,12 +85,10 @@ def tile_siglipencoderlayer_pa_kernel(
             nc.sync.dma_start(out=bias_all[n][:], in_=biases[n].partition_broadcast(P))
 
         blocks = [(n, nt, i) for n in "kvq" for nt in range(N_TILES) for i in range(RUN)]
-        for i in range(TILES):
-            nc.sync.dma_start(out=x_raw[i][:], in_=x_view[:, i // MERGE, i % MERGE, :])
-            if i % PAIR == PAIR - 1:
-                for c in range(i - 1, i + 1):
-                    load_weight(*blocks[c])
-        for c in range(TILES, len(blocks)):
+        for c in range(len(blocks)):
+            if c % 2 == 0 and c < 2 * TILES:
+                i = c // 2
+                nc.sync.dma_start(out=x_raw[i][:], in_=x_view[:, i // MERGE, i % MERGE, :])
             load_weight(*blocks[c])
         for n in "kvq":
             load_bias(n)
@@ -116,9 +115,25 @@ def tile_siglipencoderlayer_pa_kernel(
             for u in range(2):
                 nc.tensor.transpose(out=bank[:, u * P : (u + 1) * P], in_=words[:, u, :], identity=ident[:])
             src = bank[:].bitcast(BF16)[:, 0 : 4 * P].rearrange("p (u c e) -> p c u e", u=2, e=2)
-            nc.vector.tensor_copy(
+            nc.scalar.copy(
                 out=gain_bias[:].rearrange("p (c u e) -> p c u e", u=2, e=2), in_=src[:, 0 : 2 * PASSES, :, :]
             )
+
+        sorted_words = {}
+
+        def sort_weight(n, nt, i, engine="scalar"):
+            tile_ = sortp.tile([P, RUN * P], F32, tag="sorted")
+            sorted_words[(n, nt, i)] = tile_
+            dst = tile_[:].rearrange("p (g u q) -> p g u q", g=PASSES, u=2)
+            src = w_raw[n][:, nt, i * D : (i + 1) * D].bitcast(F32).rearrange(
+                "p (g q u) -> p g u q", g=PASSES, u=2
+            )
+            if engine == "vector":
+                nc.vector.tensor_copy(out=dst, in_=src)
+            elif engine == "scalar":
+                nc.scalar.copy(out=dst, in_=src)
+            else:
+                nc.gpsimd.tensor_copy(out=dst.bitcast(mybir.dt.int32), in_=src.bitcast(mybir.dt.int32))
 
         def flip_weight(n, nt, i, engine="scalar"):
             if i == 0:
@@ -133,9 +148,11 @@ def tile_siglipencoderlayer_pa_kernel(
             )
             bank = banks.tile([P, N_TILE], F32, tag="bank")
             for c in range(PASSES * 2):
-                nc.tensor.transpose(
-                    out=bank[:, c * P : (c + 1) * P], in_=words_in[:, i, c // 2, c % 2, :], identity=ident[:]
-                )
+                if (n, nt, i) in sorted_words:
+                    src = sorted_words[(n, nt, i)][:, c * P : (c + 1) * P]
+                else:
+                    src = words_in[:, i, c // 2, c % 2, :]
+                nc.tensor.transpose(out=bank[:, c * P : (c + 1) * P], in_=src, identity=ident[:])
             dst = words_out[:, :, i * P : (i + 1) * P, :]
             src = bank[:].rearrange("p (g u e) -> p g e u", g=PASSES, u=2)
             if engine == "vector":
@@ -283,9 +300,9 @@ def tile_siglipencoderlayer_pa_kernel(
             nc.sync.dma_start(out=merged_views[n][:, h, cols], in_=rows[:])
 
 
-        def weights_run(first, last, vector=()):
+        def weights_run(first, last):
             for c in range(first, last):
-                flip_weight(*blocks[c], engine="vector" if c in vector else "scalar")
+                flip_weight(*blocks[c])
 
         def stats(u):
             join_moments(2 * u)
@@ -301,72 +318,98 @@ def tile_siglipencoderlayer_pa_kernel(
             group_tokens(u, 1)
             pack_tokens(u)
 
+        def sort_run(first, last, engine="scalar"):
+            for c in range(first, last):
+                sort_weight(*blocks[c], engine)
+
         measure_tile(0)
-        weights_run(0, 1)
+        join_moments(0)
+        weights_run(0, 2)
+        flip_gain_bias()
         measure_tile(1)
-        weights_run(1, 2)
-        stats(0)
+        join_moments(1)
+        weights_run(2, 3)
+        finish_measure(0)
+        weights_run(3, 4)
         measure_tile(2)
+        weights_run(4, 6)
+        pack_weight("k", 0)
         normalise(0)
         normalise(1)
-        weights_run(2, 4)
-        flip_gain_bias()
-        measure_tile(3)
-        stats(1)
+        weights_run(6, 8)
         tokens(0)
+        join_moments(2)
+        measure_tile(3)
+        pack_weight("k", 1)
+        join_moments(3)
+        finish_measure(1)
+        weights_run(8, 12)
         measure_tile(4)
+        group_tokens(0, 0)
+        group_tokens(0, 1)
+        join_moments(4)
+        measure_tile(5)
+        pack_tokens(0)
         normalise(2)
         normalise(3)
-        weights_run(4, 8)
-        measure_tile(5)
-        stats(2)
-        tokens(1)
-        pack(0)
-        pack_weight("k", 0)
+        join_moments(5)
+        weights_run(12, 16)
+        merged("k", 0, 0, 0)
+        finish_measure(2)
+        pack_weight("v", 0)
         measure_tile(6)
-        weights_run(8, 14)
         normalise(4)
         normalise(5)
+        join_moments(6)
         measure_tile(7)
-        stats(3)
-        merged("k", 0, 0, 0)
-        weights_run(14, 18)
+        sort_run(16, 20)
+        tokens(1)
+        join_moments(7)
+        merged("k", 0, 1, 0)
         tokens(2)
-        pack(1)
-        pack_weight("k", 1)
-        pack_weight("v", 0)
+        group_tokens(1, 0)
+        group_tokens(1, 1)
+        finish_measure(3)
+        pack_weight("v", 1)
+        pack_tokens(1)
+        group_tokens(2, 0)
+        group_tokens(2, 1)
+        pack_tokens(2)
+        weights_run(16, 20)
+        sort_run(20, 24)
         normalise(6)
         normalise(7)
-        weights_run(18, 21)
-        merged("k", 0, 1, 0)
-        weights_run(21, 24)
-        tokens(3)
-        pack_weight("v", 1)
+        merged("v", 0, 0, 0)
         merged("k", 0, 0, 1)
         merged("k", 0, 1, 1)
-        pack(2)
-        merged("v", 0, 0, 0)
-        merged("v", 0, 0, 1)
         settle("k", 0, 0)
-        pack_weight("q", 0)
-        merged("v", 0, 1, 0)
-        merged("v", 0, 1, 1)
         settle("k", 0, 1)
-        pack(3)
         merged("k", 1, 0, 0)
         merged("k", 1, 1, 0)
+        pack_weight("q", 0)
+        tokens(3)
+        weights_run(20, 24)
+        merged("v", 0, 0, 1)
+        merged("v", 0, 1, 0)
+        merged("v", 1, 0, 0)
+        group_tokens(3, 0)
+        group_tokens(3, 1)
+        pack_tokens(3)
         settle("v", 0, 0)
-        pack_weight("q", 1)
-        settle("v", 0, 1)
         merged("k", 1, 0, 1)
-        settle("k", 1, 0)
         merged("k", 1, 1, 1)
+        pack_weight("q", 1)
+        settle("k", 1, 0)
         settle("k", 1, 1)
+        merged("v", 1, 0, 1)
+        merged("v", 0, 1, 1)
+        settle("v", 1, 0)
+        settle("v", 0, 1)
         for i in range(8):
             queries(i, 0)
-            if i % 4 == 3:
-                merged("v", 1, i // 4, 0)
-                merged("v", 1, i // 4, 1)
-                settle("v", 1, i // 4)
+            if i == 3:
+                merged("v", 1, 1, 0)
+                merged("v", 1, 1, 1)
+                settle("v", 1, 1)
         for i in range(8):
             queries(i, 1)

@@ -39,7 +39,7 @@ def tile_siglipencoderlayer_pa_kernel(
     tc, x, ln1_g, ln1_b, Wq, bq, Wk, bk, Wv, bv, out_0, out_1, out_2
 ):
     nc = tc.nc
-    x_view = x.flatten_outer_dims().rearrange("(h j r) d -> j h r d", h=HALVES, r=MERGE)
+    x_view = x.flatten_outer_dims().rearrange("(h j r) d -> j h (r d)", h=HALVES, r=MERGE)
     q_view = out_0.flatten_outer_dims().rearrange("(h j r) e -> j h r e", h=HALVES, r=MERGE)
     merged_views = {
         "k": out_1.flatten_outer_dims().rearrange("(h j) e -> j h e", h=HALVES),
@@ -73,23 +73,42 @@ def tile_siglipencoderlayer_pa_kernel(
         nc.scalar.dma_start(out=gb_rows[0:PASSES, :], in_=ln1_g.rearrange("(c w) -> c w", c=PASSES))
         nc.scalar.dma_start(out=gb_rows[PASSES : 2 * PASSES, :], in_=ln1_b.rearrange("(c w) -> c w", c=PASSES))
 
-        x_raw = [raw.tile([P, D], BF16, name="x_raw%d" % i) for i in range(TILES)]
+        x_raw = [raw.tile([P, PAIR * D], BF16, name="x_raw%d" % u) for u in range(UNITS)]
         w_raw = {n: raw.tile([P, N_TILES, RUN * D], BF16, name="w_raw_" + n) for n in "qkv"}
         bias_all = {n: consts.tile([P, E], BF16, name="bias_all_" + n) for n in "qkv"}
 
-        def load_weight(n, nt, i):
-            rows = weights[n].rearrange("(nt i p) d -> p nt i d", nt=N_TILES, p=P)
-            nc.sync.dma_start(out=w_raw[n][:, nt, i * D : (i + 1) * D], in_=rows[:, nt, i, :])
+        def load_tokens(u, first, count):
+            src = slice((u % (UNITS // HALVES) * PAIR + first) * D, (u % (UNITS // HALVES) * PAIR + first + count) * D)
+            nc.sync.dma_start(
+                out=x_raw[u][:, first * D : (first + count) * D], in_=x_view[:, u // (UNITS // HALVES), src]
+            )
+
+        def load_weights(n, nt, first, count):
+            rows = weights[n].rearrange("(nt p i) d -> p nt (i d)", nt=N_TILES, i=RUN)
+            cols = slice(first * D, (first + count) * D)
+            nc.sync.dma_start(out=w_raw[n][:, nt, cols], in_=rows[:, nt, cols])
 
         def load_bias(n):
             nc.sync.dma_start(out=bias_all[n][:], in_=biases[n].partition_broadcast(P))
 
         blocks = [(n, nt, i) for n in "kvq" for nt in range(N_TILES) for i in range(RUN)]
-        for c in range(len(blocks)):
-            if c % 2 == 0 and c < 2 * TILES:
-                i = c // 2
-                nc.sync.dma_start(out=x_raw[i][:], in_=x_view[:, i // MERGE, i % MERGE, :])
-            load_weight(*blocks[c])
+        blocks = [(n, nt, i) for n in "kvq" for nt in range(N_TILES) for i in range(RUN)]
+        load_tokens(0, 0, 1)
+        load_weights("k", 0, 0, 1)
+        load_tokens(0, 1, 1)
+        load_weights("k", 0, 1, 1)
+        load_weights("k", 0, 2, 2)
+        load_tokens(1, 0, PAIR)
+        load_weights("k", 1, 0, 2)
+        load_weights("k", 1, 2, 2)
+        load_weights("v", 0, 0, 2)
+        load_tokens(2, 0, PAIR)
+        load_weights("v", 0, 2, 2)
+        load_weights("v", 1, 0, 2)
+        load_tokens(3, 0, PAIR)
+        load_weights("v", 1, 2, 2)
+        load_weights("q", 0, 0, RUN)
+        load_weights("q", 1, 0, RUN)
         for n in "kvq":
             load_bias(n)
 
@@ -173,7 +192,7 @@ def tile_siglipencoderlayer_pa_kernel(
             stats = small.tile([P, D // BN_MAX, 6], F32, tag="stats")
             stats_tiles[i] = stats
             for s in range(D // BN_MAX):
-                nc.vector.bn_stats(out=stats[:, s, :], in_=x_raw[i][:, s * BN_MAX : (s + 1) * BN_MAX])
+                nc.vector.bn_stats(out=stats[:, s, :], in_=x_raw[i // PAIR][:, i % PAIR * D + s * BN_MAX : i % PAIR * D + (s + 1) * BN_MAX])
 
         def join_moments(i):
             u = i // PAIR
@@ -198,7 +217,7 @@ def tile_siglipencoderlayer_pa_kernel(
             xn = normed.tile([P, D], F32, tag="xn")
             xn_tiles[i] = xn
             dst = xn[:].rearrange("p (g t q) -> p g t q", g=PASSES, t=PACK)
-            src = x_raw[i][:].rearrange("p (g q t) -> p g t q", g=PASSES, t=PACK)
+            src = x_raw[u][:, r * D : (r + 1) * D].rearrange("p (g q t) -> p g t q", g=PASSES, t=PACK)
             if True:
                 eng = nc.vector if engine == "vector" else nc.gpsimd
                 eng.tensor_scalar(
@@ -268,14 +287,23 @@ def tile_siglipencoderlayer_pa_kernel(
                 stop=stop,
             )
 
+        def by_feature(acc):
+            return acc[:].rearrange("q (i p) -> q p i", i=RUN)
+
+        def natural(tile_, nt=0):
+            return tile_[:, nt * N_TILE : (nt + 1) * N_TILE].rearrange("q (p i) -> q p i", i=RUN)
+
         def queries(i, nt):
-            cols = slice(nt * N_TILE, (nt + 1) * N_TILE)
             acc = banks.tile([P, N_TILE], F32, tag="bank")
             for g in range(PASSES):
                 one_pass(acc, "q", i, g, nt, g == 0, g == PASSES - 1)
             rows = results.tile([P, N_TILE], F32, tag="rows")
-            nc.vector.tensor_tensor(out=rows[:], in0=acc[:], in1=bias_all["q"][:, cols], op=ALU.add)
-            nc.sync.dma_start(out=q_view[:, i // MERGE, i % MERGE, cols], in_=rows[:])
+            nc.vector.tensor_tensor(
+                out=natural(rows), in0=by_feature(acc), in1=natural(bias_all["q"], nt), op=ALU.add
+            )
+            nc.sync.dma_start(
+                out=q_view[:, i // MERGE, i % MERGE, nt * N_TILE : (nt + 1) * N_TILE], in_=rows[:]
+            )
 
         accs = {}
 
@@ -294,7 +322,7 @@ def tile_siglipencoderlayer_pa_kernel(
             cols = slice(nt * N_TILE, (nt + 1) * N_TILE)
             rows = results.tile([P, N_TILE], F32, tag="rows")
             nc.vector.scalar_tensor_tensor(
-                out=rows[:], in0=accs[(n, h, nt)][:], scalar=1.0 / MERGE, in1=bias_all[n][:, cols],
+                out=natural(rows), in0=by_feature(accs[(n, h, nt)]), scalar=1.0 / MERGE, in1=natural(bias_all[n], nt),
                 op0=ALU.mult, op1=ALU.add,
             )
             nc.sync.dma_start(out=merged_views[n][:, h, cols], in_=rows[:])
@@ -324,92 +352,88 @@ def tile_siglipencoderlayer_pa_kernel(
 
         measure_tile(0)
         join_moments(0)
-        weights_run(0, 2)
+        weights_run(0, 1)
         flip_gain_bias()
         measure_tile(1)
         join_moments(1)
-        weights_run(2, 3)
+        weights_run(1, 2)
         finish_measure(0)
-        weights_run(3, 4)
-        measure_tile(2)
-        weights_run(4, 6)
-        pack_weight("k", 0)
+        weights_run(2, 4)
         normalise(0)
         normalise(1)
-        weights_run(6, 8)
+        measure_tile(2)
         tokens(0)
         join_moments(2)
+        pack_weight("k", 0)
         measure_tile(3)
-        pack_weight("k", 1)
         join_moments(3)
-        finish_measure(1)
-        weights_run(8, 12)
-        measure_tile(4)
         group_tokens(0, 0)
         group_tokens(0, 1)
-        join_moments(4)
-        measure_tile(5)
+        weights_run(4, 8)
+        finish_measure(1)
+        measure_tile(4)
         pack_tokens(0)
+        join_moments(4)
+        weights_run(8, 12)
         normalise(2)
         normalise(3)
+        pack_weight("k", 1)
+        measure_tile(5)
         join_moments(5)
-        weights_run(12, 16)
         merged("k", 0, 0, 0)
-        finish_measure(2)
+        tokens(1)
         pack_weight("v", 0)
+        finish_measure(2)
         measure_tile(6)
         normalise(4)
         normalise(5)
-        join_moments(6)
-        measure_tile(7)
-        sort_run(16, 20)
-        tokens(1)
-        join_moments(7)
+        weights_run(12, 16)
+        sort_run(16, 18)
         merged("k", 0, 1, 0)
-        tokens(2)
         group_tokens(1, 0)
         group_tokens(1, 1)
-        finish_measure(3)
-        pack_weight("v", 1)
+        measure_tile(7)
+        join_moments(6)
         pack_tokens(1)
-        group_tokens(2, 0)
-        group_tokens(2, 1)
-        pack_tokens(2)
-        weights_run(16, 20)
-        sort_run(20, 24)
+        join_moments(7)
+        sort_run(18, 20)
+        finish_measure(3)
+        merged("v", 0, 0, 0)
+        tokens(2)
+        pack_weight("v", 1)
         normalise(6)
         normalise(7)
-        merged("v", 0, 0, 0)
         merged("k", 0, 0, 1)
         merged("k", 0, 1, 1)
-        settle("k", 0, 0)
-        settle("k", 0, 1)
-        merged("k", 1, 0, 0)
-        merged("k", 1, 1, 0)
-        pack_weight("q", 0)
+        group_tokens(2, 0)
+        group_tokens(2, 1)
         tokens(3)
-        weights_run(20, 24)
+        weights_run(16, 20)
+        sort_run(20, 24)
+        settle("k", 0, 0)
+        pack_tokens(2)
+        settle("k", 0, 1)
         merged("v", 0, 0, 1)
         merged("v", 0, 1, 0)
-        merged("v", 1, 0, 0)
         group_tokens(3, 0)
         group_tokens(3, 1)
+        pack_weight("q", 0)
+        merged("v", 0, 1, 1)
         pack_tokens(3)
         settle("v", 0, 0)
+        merged("k", 1, 0, 0)
+        settle("v", 0, 1)
+        weights_run(20, 24)
         merged("k", 1, 0, 1)
-        merged("k", 1, 1, 1)
         pack_weight("q", 1)
         settle("k", 1, 0)
-        settle("k", 1, 1)
-        merged("v", 1, 0, 1)
-        merged("v", 0, 1, 1)
-        settle("v", 1, 0)
-        settle("v", 0, 1)
-        for i in range(8):
-            queries(i, 0)
-            if i == 3:
-                merged("v", 1, 1, 0)
-                merged("v", 1, 1, 1)
-                settle("v", 1, 1)
-        for i in range(8):
-            queries(i, 1)
+        parts = [(n, nt, part) for n in "kv" for nt in range(N_TILES) for part in range(2)]
+        def tail_part(j):
+            n, nt, part = parts[j]
+            merged(n, 1, nt, part)
+            if part == 1:
+                settle(n, 1, nt)
+        for j in range(2 * TILES):
+            queries(j % TILES, j // TILES)
+            if j % 2 and j > 3:
+                tail_part(j // 2)

@@ -63,15 +63,15 @@ def tile_siglipencoderlayer_pa_kernel(
 
         ident = consts.tile([P, P], F32, name="ident")
         make_identity(nc, ident[:])
+        gb_rows = consts.tile([P, K_PASS], BF16, name="gb_rows")
+        nc.vector.memset(gb_rows[:], 0.0)
+        nc.scalar.dma_start(out=gb_rows[0:PASSES, :], in_=ln1_g.rearrange("(c w) -> c w", c=PASSES))
+        nc.scalar.dma_start(out=gb_rows[PASSES : 2 * PASSES, :], in_=ln1_b.rearrange("(c w) -> c w", c=PASSES))
         eps = consts.tile([P, 1], F32, name="eps")
         nc.vector.memset(eps[:], EPS)
         warm = consts.tile([P, 1], F32, name="warm")
         nc.scalar.activation(out=warm[:], in_=eps[:], func=ACT.Abs_reciprocal_sqrt)
 
-        gb_rows = consts.tile([P, K_PASS], BF16, name="gb_rows")
-        nc.vector.memset(gb_rows[:], 0.0)
-        nc.scalar.dma_start(out=gb_rows[0:PASSES, :], in_=ln1_g.rearrange("(c w) -> c w", c=PASSES))
-        nc.scalar.dma_start(out=gb_rows[PASSES : 2 * PASSES, :], in_=ln1_b.rearrange("(c w) -> c w", c=PASSES))
 
         x_raw = [raw.tile([P, PAIR * D], BF16, name="x_raw%d" % u) for u in range(UNITS)]
         w_raw = {n: raw.tile([P, N_TILES, RUN * D], BF16, name="w_raw_" + n) for n in "qkv"}
@@ -353,43 +353,44 @@ def tile_siglipencoderlayer_pa_kernel(
         measure_tile(0)
         join_moments(0)
         weights_run(0, 1)
-        flip_gain_bias()
         measure_tile(1)
         join_moments(1)
-        weights_run(1, 2)
         finish_measure(0)
-        weights_run(2, 4)
+        weights_run(1, 4)
         normalise(0)
         normalise(1)
+        flip_gain_bias()
         measure_tile(2)
         tokens(0)
+        weights_run(4, 6)
+        measure_tile(3)
         join_moments(2)
         pack_weight("k", 0)
-        measure_tile(3)
         join_moments(3)
+        weights_run(6, 8)
         group_tokens(0, 0)
         group_tokens(0, 1)
-        weights_run(4, 8)
+        weights_run(8, 10)
         finish_measure(1)
         measure_tile(4)
         pack_tokens(0)
-        join_moments(4)
-        weights_run(8, 12)
         normalise(2)
         normalise(3)
-        pack_weight("k", 1)
         measure_tile(5)
+        weights_run(10, 12)
+        join_moments(4)
+        pack_weight("k", 1)
         join_moments(5)
+        weights_run(12, 13)
         merged("k", 0, 0, 0)
         tokens(1)
-        pack_weight("v", 0)
         finish_measure(2)
+        pack_weight("v", 0)
         measure_tile(6)
         normalise(4)
         normalise(5)
-        weights_run(12, 16)
         sort_run(16, 18)
-        merged("k", 0, 1, 0)
+        weights_run(13, 16)
         group_tokens(1, 0)
         group_tokens(1, 1)
         measure_tile(7)
@@ -398,42 +399,62 @@ def tile_siglipencoderlayer_pa_kernel(
         join_moments(7)
         sort_run(18, 20)
         finish_measure(3)
-        merged("v", 0, 0, 0)
-        tokens(2)
+        merged("k", 0, 1, 0)
         pack_weight("v", 1)
+        tokens(2)
         normalise(6)
         normalise(7)
+        merged("v", 0, 0, 0)
         merged("k", 0, 0, 1)
         merged("k", 0, 1, 1)
         group_tokens(2, 0)
         group_tokens(2, 1)
+        weights_run(16, 18)
         tokens(3)
-        weights_run(16, 20)
-        sort_run(20, 24)
-        settle("k", 0, 0)
+        weights_run(18, 20)
         pack_tokens(2)
+        settle("k", 0, 0)
         settle("k", 0, 1)
         merged("v", 0, 0, 1)
         merged("v", 0, 1, 0)
+        sort_run(20, 24)
         group_tokens(3, 0)
         group_tokens(3, 1)
         pack_weight("q", 0)
-        merged("v", 0, 1, 1)
         pack_tokens(3)
-        settle("v", 0, 0)
+        merged("v", 0, 1, 1)
         merged("k", 1, 0, 0)
+        settle("v", 0, 0)
         settle("v", 0, 1)
         weights_run(20, 24)
-        merged("k", 1, 0, 1)
-        pack_weight("q", 1)
-        settle("k", 1, 0)
         parts = [(n, nt, part) for n in "kv" for nt in range(N_TILES) for part in range(2)]
         def tail_part(j):
             n, nt, part = parts[j]
             merged(n, 1, nt, part)
             if part == 1:
                 settle(n, 1, nt)
-        for j in range(2 * TILES):
-            queries(j % TILES, j // TILES)
-            if j % 2 and j > 3:
-                tail_part(j // 2)
+
+        queries(0, 0)
+        queries(1, 0)
+        queries(2, 0)
+        queries(3, 0)
+        tail_part(1)
+        pack_weight("q", 1)
+        tail_part(2)
+        queries(4, 0)
+        queries(5, 0)
+        tail_part(3)
+        queries(6, 0)
+        queries(7, 0)
+        tail_part(4)
+        queries(0, 1)
+        queries(1, 1)
+        tail_part(5)
+        queries(2, 1)
+        queries(3, 1)
+        queries(4, 1)
+        tail_part(6)
+        queries(5, 1)
+        queries(6, 1)
+        queries(7, 1)
+        tail_part(7)

@@ -216,8 +216,8 @@ def tile_siglipencoderlayer_pa_kernel(
             rstd = rstds[u]
             xn = normed.tile([P, D], F32, tag="xn")
             xn_tiles[i] = xn
-            dst = xn[:].rearrange("p (g t q) -> p g t q", g=PASSES, t=PACK)
-            src = x_raw[u][:, r * D : (r + 1) * D].rearrange("p (g q t) -> p g t q", g=PASSES, t=PACK)
+            dst = xn[:].rearrange("p (g t q) -> p g q t", g=PASSES, t=PACK)
+            src = x_raw[u][:, r * D : (r + 1) * D].rearrange("p (g q t) -> p g q t", g=PASSES, t=PACK)
             if True:
                 eng = nc.vector if engine == "vector" else nc.gpsimd
                 eng.tensor_scalar(
@@ -260,8 +260,8 @@ def tile_siglipencoderlayer_pa_kernel(
         def group_tokens(u, g, engine="vector"):
             if g == 0:
                 h_grouped[u] = grouped.tile([P, PASSES, UNIT * PACK], BF16, name="h_grouped", tag="h_grouped", align_bytes=64)
-            dst = h_grouped[u][:, g, :].rearrange("p (n t) -> p n t", t=PACK)
-            src = h_plane[u][:, g * PACK : (g + 1) * PACK, :].rearrange("p t n -> p n t")
+            dst = h_grouped[u][:, g, :].rearrange("p (c i t) -> p c t i", i=PACK, t=PACK)
+            src = h_plane[u][:, g * PACK : (g + 1) * PACK, :].rearrange("p t (c i) -> p c t i", i=PACK)
             if engine == "vector":
                 nc.vector.tensor_copy(out=dst, in_=src)
             else:

@@ -32,6 +32,8 @@ N_TILES = E // N_TILE
 RUN = N_TILE // P
 BN_MAX = 512
 
+LAST = ("v", 1)
+
 FLOPS = 2 * 3 * TOKENS * D * E
 
 
@@ -126,6 +128,7 @@ def tile_siglipencoderlayer_pa_kernel(
         w_grouped = {}
         xn_tiles = {}
         rstds = {}
+        shifts = {}
         mean_vars = {}
 
         def flip_gain_bias():
@@ -137,6 +140,9 @@ def tile_siglipencoderlayer_pa_kernel(
             nc.scalar.copy(
                 out=gain_bias[:].rearrange("p (c u e) -> p c u e", u=2, e=2), in_=src[:, 0 : 2 * PASSES, :, :]
             )
+
+        def parts_of(n, nt):
+            return 2 if (n, nt) == LAST else 1
 
         sorted_words = {}
 
@@ -172,12 +178,17 @@ def tile_siglipencoderlayer_pa_kernel(
                 else:
                     src = words_in[:, i, c // 2, c % 2, :]
                 nc.tensor.transpose(out=bank[:, c * P : (c + 1) * P], in_=src, identity=ident[:])
-            dst = words_out[:, :, i * P : (i + 1) * P, :]
             src = bank[:].rearrange("p (g u e) -> p g e u", g=PASSES, u=2)
-            if engine == "vector":
-                nc.vector.tensor_copy(out=dst, in_=src)
-            else:
-                nc.scalar.copy(out=dst, in_=src)
+            parts = parts_of(n, nt)
+            width = P // parts
+            for s in range(parts):
+                first = (s * RUN + i) * width
+                dst = words_out[:, :, first : first + width, :]
+                part_src = src[:, :, s * width : (s + 1) * width, :]
+                if engine == "vector":
+                    nc.vector.tensor_copy(out=dst, in_=part_src)
+                else:
+                    nc.scalar.copy(out=dst, in_=part_src)
 
         def pack_weight(n, nt):
             nc.vector.quantize_mx(
@@ -210,6 +221,14 @@ def tile_siglipencoderlayer_pa_kernel(
             )
             rstds[u] = rstd
 
+        def finish_shift(u):
+            shift = small.tile([P, PAIR], F32, tag="shift")
+            nc.vector.scalar_tensor_tensor(
+                out=shift[:], in0=mean_vars[u][:, :, 0], scalar=-1.0, in1=rstds[u][:],
+                op0=ALU.mult, op1=ALU.mult,
+            )
+            shifts[u] = shift
+
 
         def normalise(i, engine="vector"):
             u, r = i // PAIR, i % PAIR
@@ -218,7 +237,11 @@ def tile_siglipencoderlayer_pa_kernel(
             xn_tiles[i] = xn
             dst = xn[:].rearrange("p (g t q) -> p g q t", g=PASSES, t=PACK)
             src = x_raw[u][:, r * D : (r + 1) * D].rearrange("p (g q t) -> p g q t", g=PASSES, t=PACK)
-            if True:
+            if engine == "scalar":
+                nc.scalar.activation(
+                    out=dst, in_=src, func=ACT.Identity, scale=rstd[:, r : r + 1], bias=shifts[u][:, r : r + 1]
+                )
+            else:
                 eng = nc.vector if engine == "vector" else nc.gpsimd
                 eng.tensor_scalar(
                     out=dst, in0=src, scalar1=mean_vars[u][:, r, 0:1], scalar2=rstd[:, r : r + 1],
@@ -273,12 +296,12 @@ def tile_siglipencoderlayer_pa_kernel(
                 in_=h_grouped[u][:].rearrange("p g w -> p (g w)"),
             )
 
-        def one_pass(acc, n, i, g, nt, start, stop):
+        def one_pass(acc, n, i, g, nt, start, stop, first=0, width=N_TILE):
             u = i // PAIR
             toks = slice(g * UNIT + (i % PAIR) * P, g * UNIT + (i % PAIR) * P + P)
-            cols = slice(g * N_TILE, (g + 1) * N_TILE)
+            cols = slice(g * N_TILE + first, g * N_TILE + first + width)
             nc.tensor.matmul_mx(
-                out=acc[:],
+                out=acc[:, first : first + width],
                 lhsT=h_words[:, u, toks].bitcast(FP8X4),
                 lhsT_scale=h_scales[:, u, toks],
                 rhs=w_words[n][:, nt, cols].bitcast(FP8X4),
@@ -287,11 +310,11 @@ def tile_siglipencoderlayer_pa_kernel(
                 stop=stop,
             )
 
-        def by_feature(acc):
-            return acc[:].rearrange("q (i p) -> q p i", i=RUN)
+        def by_feature(acc, first=0, width=N_TILE):
+            return acc[:, first : first + width].rearrange("q (i p) -> q p i", i=RUN)
 
-        def natural(tile_, nt=0):
-            return tile_[:, nt * N_TILE : (nt + 1) * N_TILE].rearrange("q (p i) -> q p i", i=RUN)
+        def natural(tile_, first, width=N_TILE):
+            return tile_[:, first : first + width].rearrange("q (p i) -> q p i", i=RUN)
 
         def queries(i, nt):
             acc = banks.tile([P, N_TILE], F32, tag="bank")
@@ -299,7 +322,7 @@ def tile_siglipencoderlayer_pa_kernel(
                 one_pass(acc, "q", i, g, nt, g == 0, g == PASSES - 1)
             rows = results.tile([P, N_TILE], F32, tag="rows")
             nc.vector.tensor_tensor(
-                out=natural(rows), in0=by_feature(acc), in1=natural(bias_all["q"], nt), op=ALU.add
+                out=natural(rows, 0), in0=by_feature(acc), in1=natural(bias_all["q"], nt * N_TILE), op=ALU.add
             )
             nc.sync.dma_start(
                 out=q_view[:, i // MERGE, i % MERGE, nt * N_TILE : (nt + 1) * N_TILE], in_=rows[:]
@@ -319,13 +342,35 @@ def tile_siglipencoderlayer_pa_kernel(
                     )
 
         def settle(n, h, nt):
-            cols = slice(nt * N_TILE, (nt + 1) * N_TILE)
+            width = N_TILE // parts_of(n, nt)
             rows = results.tile([P, N_TILE], F32, tag="rows")
-            nc.vector.scalar_tensor_tensor(
-                out=natural(rows), in0=by_feature(accs[(n, h, nt)]), scalar=1.0 / MERGE, in1=natural(bias_all[n], nt),
-                op0=ALU.mult, op1=ALU.add,
-            )
-            nc.sync.dma_start(out=merged_views[n][:, h, cols], in_=rows[:])
+            for first in range(0, N_TILE, width):
+                nc.vector.scalar_tensor_tensor(
+                    out=natural(rows, first, width), in0=by_feature(accs[(n, h, nt)], first, width),
+                    scalar=1.0 / MERGE, in1=natural(bias_all[n], nt * N_TILE + first, width),
+                    op0=ALU.mult, op1=ALU.add,
+                )
+            nc.sync.dma_start(out=merged_views[n][:, h, nt * N_TILE : (nt + 1) * N_TILE], in_=rows[:])
+
+        def last_products(h):
+            n, nt = LAST
+            half = N_TILE // 2
+            for s in range(2):
+                acc = banks.tile([P, N_TILE], F32, name="acc", tag="bank")
+                for i in range(h * MERGE, (h + 1) * MERGE):
+                    for g in range(PASSES):
+                        one_pass(
+                            acc, n, i, g, nt, i == h * MERGE and g == 0,
+                            i == (h + 1) * MERGE - 1 and g == PASSES - 1, s * half, half,
+                        )
+                rows = results.tile([P, half], F32, name="half_rows", tag="half_rows")
+                nc.vector.scalar_tensor_tensor(
+                    out=natural(rows, 0, half), in0=by_feature(acc, s * half, half), scalar=1.0 / MERGE,
+                    in1=natural(bias_all[n], nt * N_TILE + s * half, half), op0=ALU.mult, op1=ALU.add,
+                )
+                nc.sync.dma_start(
+                    out=merged_views[n][:, h, nt * N_TILE + s * half : nt * N_TILE + (s + 1) * half], in_=rows[:]
+                )
 
 
         def weights_run(first, last):
@@ -351,82 +396,82 @@ def tile_siglipencoderlayer_pa_kernel(
                 sort_weight(*blocks[c], engine)
 
         measure_tile(0)
-        join_moments(0)
         weights_run(0, 1)
         measure_tile(1)
+        join_moments(0)
         join_moments(1)
         finish_measure(0)
         weights_run(1, 4)
         normalise(0)
         normalise(1)
         flip_gain_bias()
-        measure_tile(2)
         tokens(0)
-        weights_run(4, 6)
+        measure_tile(2)
+        pack_weight("k", 0)
         measure_tile(3)
         join_moments(2)
-        pack_weight("k", 0)
         join_moments(3)
-        weights_run(6, 8)
+        weights_run(4, 7)
         group_tokens(0, 0)
         group_tokens(0, 1)
-        weights_run(8, 10)
         finish_measure(1)
         measure_tile(4)
+        finish_shift(1)
+        weights_run(7, 10)
         pack_tokens(0)
-        normalise(2)
-        normalise(3)
         measure_tile(5)
         weights_run(10, 12)
         join_moments(4)
-        pack_weight("k", 1)
+        normalise(3, "scalar")
+        normalise(2)
         join_moments(5)
-        weights_run(12, 13)
+        weights_run(12, 14)
         merged("k", 0, 0, 0)
-        tokens(1)
         finish_measure(2)
         pack_weight("v", 0)
-        measure_tile(6)
+        tokens(1)
+        sort_run(16, 17)
+        pack_weight("k", 1)
         normalise(4)
         normalise(5)
-        sort_run(16, 18)
-        weights_run(13, 16)
         group_tokens(1, 0)
         group_tokens(1, 1)
+        weights_run(14, 16)
+        sort_run(17, 19)
+        merged("k", 0, 1, 0)
+        merged("v", 0, 0, 0)
+        measure_tile(6)
+        pack_tokens(1)
         measure_tile(7)
         join_moments(6)
-        pack_tokens(1)
         join_moments(7)
-        sort_run(18, 20)
+        sort_run(19, 20)
         finish_measure(3)
-        merged("k", 0, 1, 0)
-        pack_weight("v", 1)
+        weights_run(16, 17)
         tokens(2)
+        pack_weight("v", 1)
         normalise(6)
         normalise(7)
-        merged("v", 0, 0, 0)
         merged("k", 0, 0, 1)
         merged("k", 0, 1, 1)
         group_tokens(2, 0)
         group_tokens(2, 1)
-        weights_run(16, 18)
-        tokens(3)
-        weights_run(18, 20)
-        pack_tokens(2)
+        weights_run(17, 20)
+        sort_run(20, 21)
         settle("k", 0, 0)
+        pack_tokens(2)
         settle("k", 0, 1)
+        tokens(3)
+        sort_run(21, 24)
+        pack_weight("q", 0)
         merged("v", 0, 0, 1)
         merged("v", 0, 1, 0)
-        sort_run(20, 24)
-        group_tokens(3, 0)
-        group_tokens(3, 1)
-        pack_weight("q", 0)
-        pack_tokens(3)
         merged("v", 0, 1, 1)
         merged("k", 1, 0, 0)
         settle("v", 0, 0)
         settle("v", 0, 1)
-        weights_run(20, 24)
+        group_tokens(3, 0)
+        group_tokens(3, 1)
         parts = [(n, nt, part) for n in "kv" for nt in range(N_TILES) for part in range(2)]
         def tail_part(j):
             n, nt, part = parts[j]
@@ -437,24 +482,25 @@ def tile_siglipencoderlayer_pa_kernel(
         queries(0, 0)
         queries(1, 0)
         queries(2, 0)
+        weights_run(20, 24)
+        pack_tokens(3)
         queries(3, 0)
-        tail_part(1)
-        pack_weight("q", 1)
-        tail_part(2)
         queries(4, 0)
         queries(5, 0)
-        tail_part(3)
+        pack_weight("q", 1)
+        tail_part(1)
+        tail_part(2)
         queries(6, 0)
         queries(7, 0)
-        tail_part(4)
+        tail_part(3)
         queries(0, 1)
         queries(1, 1)
-        tail_part(5)
+        tail_part(4)
         queries(2, 1)
         queries(3, 1)
         queries(4, 1)
-        tail_part(6)
         queries(5, 1)
+        tail_part(5)
         queries(6, 1)
         queries(7, 1)
-        tail_part(7)
+        last_products(1)

@@ -407,8 +407,8 @@ def tile_siglipencoderlayer_pa_kernel(
         flip_gain_bias()
         tokens(0)
         measure_tile(2)
-        pack_weight("k", 0)
         measure_tile(3)
+        pack_weight("k", 0)
         join_moments(2)
         join_moments(3)
         weights_run(4, 7)
@@ -454,19 +454,19 @@ def tile_siglipencoderlayer_pa_kernel(
         normalise(7)
         merged("k", 0, 0, 1)
         merged("k", 0, 1, 1)
+        merged("v", 0, 0, 1)
+        settle("k", 0, 0)
         group_tokens(2, 0)
         group_tokens(2, 1)
         weights_run(17, 20)
         sort_run(20, 21)
-        settle("k", 0, 0)
         pack_tokens(2)
         settle("k", 0, 1)
+        merged("v", 0, 1, 0)
+        merged("v", 0, 1, 1)
         tokens(3)
         sort_run(21, 24)
         pack_weight("q", 0)
-        merged("v", 0, 0, 1)
-        merged("v", 0, 1, 0)
-        merged("v", 0, 1, 1)
         merged("k", 1, 0, 0)
         settle("v", 0, 0)
         settle("v", 0, 1)

@@ -54,10 +54,10 @@ def tile_siglipencoderlayer_pa_kernel(
         consts = stack.enter_context(tc.tile_pool(name="consts", bufs=1))
         raw = stack.enter_context(tc.tile_pool(name="raw", bufs=1))
         small = stack.enter_context(tc.tile_pool(name="small", bufs=4))
-        normed = stack.enter_context(tc.tile_pool(name="normed", bufs=TILES))
+        normed = stack.enter_context(tc.tile_pool(name="normed", bufs=6))
         planes = stack.enter_context(tc.tile_pool(name="planes", bufs=2))
         grouped = stack.enter_context(tc.tile_pool(name="grouped", bufs=4))
-        sortp = stack.enter_context(tc.tile_pool(name="sortp", bufs=4))
+        sortp = stack.enter_context(tc.tile_pool(name="sortp", bufs=2 * RUN))
         packed = stack.enter_context(tc.tile_pool(name="packed", bufs=1))
         results = stack.enter_context(tc.tile_pool(name="results", bufs=10))
         banks = stack.enter_context(tc.psum_pool(name="banks", bufs=8))
@@ -93,13 +93,10 @@ def tile_siglipencoderlayer_pa_kernel(
         def load_bias(n):
             nc.sync.dma_start(out=bias_all[n][:], in_=biases[n].partition_broadcast(P))
 
-        blocks = [(n, nt, i) for n in "kvq" for nt in range(N_TILES) for i in range(RUN)]
-        blocks = [(n, nt, i) for n in "kvq" for nt in range(N_TILES) for i in range(RUN)]
         load_tokens(0, 0, 1)
-        load_weights("k", 0, 0, 1)
         load_tokens(0, 1, 1)
-        load_weights("k", 0, 1, 1)
-        load_weights("k", 0, 2, 2)
+        for i in range(RUN):
+            load_weights("k", 0, i, 1)
         load_tokens(1, 0, PAIR)
         load_weights("k", 1, 0, 2)
         load_weights("k", 1, 2, 2)
@@ -146,21 +143,16 @@ def tile_siglipencoderlayer_pa_kernel(
 
         sorted_words = {}
 
-        def sort_weight(n, nt, i, engine="scalar"):
+        def sort_weight(n, nt, i):
             tile_ = sortp.tile([P, RUN * P], F32, tag="sorted")
             sorted_words[(n, nt, i)] = tile_
             dst = tile_[:].rearrange("p (g u q) -> p g u q", g=PASSES, u=2)
             src = w_raw[n][:, nt, i * D : (i + 1) * D].bitcast(F32).rearrange(
                 "p (g q u) -> p g u q", g=PASSES, u=2
             )
-            if engine == "vector":
-                nc.vector.tensor_copy(out=dst, in_=src)
-            elif engine == "scalar":
-                nc.scalar.copy(out=dst, in_=src)
-            else:
-                nc.gpsimd.tensor_copy(out=dst.bitcast(mybir.dt.int32), in_=src.bitcast(mybir.dt.int32))
+            nc.scalar.copy(out=dst, in_=src)
 
-        def flip_weight(n, nt, i, engine="scalar"):
+        def flip_weight(n, nt, i):
             if i == 0:
                 w_grouped[(n, nt)] = grouped.tile(
                     [P, PASSES * N_TILE * PACK], BF16, name="w_grouped", tag="w_grouped", align_bytes=64
@@ -185,10 +177,7 @@ def tile_siglipencoderlayer_pa_kernel(
                 first = (s * RUN + i) * width
                 dst = words_out[:, :, first : first + width, :]
                 part_src = src[:, :, s * width : (s + 1) * width, :]
-                if engine == "vector":
-                    nc.vector.tensor_copy(out=dst, in_=part_src)
-                else:
-                    nc.scalar.copy(out=dst, in_=part_src)
+                nc.scalar.copy(out=dst, in_=part_src)
 
         def pack_weight(n, nt):
             nc.vector.quantize_mx(
@@ -199,11 +188,13 @@ def tile_siglipencoderlayer_pa_kernel(
 
         stats_tiles = {}
 
-        def measure_tile(i):
-            stats = small.tile([P, D // BN_MAX, 6], F32, tag="stats")
-            stats_tiles[i] = stats
-            for s in range(D // BN_MAX):
-                nc.vector.bn_stats(out=stats[:, s, :], in_=x_raw[i // PAIR][:, i % PAIR * D + s * BN_MAX : i % PAIR * D + (s + 1) * BN_MAX])
+        def measure_tile(i, halves=range(D // BN_MAX)):
+            u, r = i // PAIR, i % PAIR
+            if 0 in halves:
+                stats_tiles[i] = small.tile([P, D // BN_MAX, 6], F32, name="stats", tag="stats")
+            for s in halves:
+                first = r * D + s * BN_MAX
+                nc.vector.bn_stats(out=stats_tiles[i][:, s, :], in_=x_raw[u][:, first : first + BN_MAX])
 
         def join_moments(i):
             u = i // PAIR
@@ -213,22 +204,21 @@ def tile_siglipencoderlayer_pa_kernel(
                 out=mean_vars[u][:, i % PAIR, :], in_=stats_tiles[i][:].rearrange("p s k -> p (s k)")
             )
 
-        def finish_measure(u):
-            mean_var = mean_vars[u]
-            rstd = small.tile([P, PAIR], F32, tag="rstd")
+        def invert_std(u, first=0, count=PAIR):
+            if first == 0:
+                rstds[u] = small.tile([P, PAIR], F32, name="rstd", tag="rstd")
+            tiles = slice(first, first + count)
             nc.scalar.activation(
-                out=rstd[:], in_=mean_var[:, :, 1], func=ACT.Abs_reciprocal_sqrt, bias=eps[:, 0:1]
+                out=rstds[u][:, tiles], in_=mean_vars[u][:, tiles, 1], func=ACT.Abs_reciprocal_sqrt, bias=eps[:, 0:1]
             )
-            rstds[u] = rstd
 
-        def finish_shift(u):
+        def find_shift(u):
             shift = small.tile([P, PAIR], F32, tag="shift")
             nc.vector.scalar_tensor_tensor(
                 out=shift[:], in0=mean_vars[u][:, :, 0], scalar=-1.0, in1=rstds[u][:],
                 op0=ALU.mult, op1=ALU.mult,
             )
             shifts[u] = shift
-
 
         def normalise(i, engine="vector"):
             u, r = i // PAIR, i % PAIR
@@ -242,15 +232,14 @@ def tile_siglipencoderlayer_pa_kernel(
                     out=dst, in_=src, func=ACT.Identity, scale=rstd[:, r : r + 1], bias=shifts[u][:, r : r + 1]
                 )
             else:
-                eng = nc.vector if engine == "vector" else nc.gpsimd
-                eng.tensor_scalar(
+                nc.vector.tensor_scalar(
                     out=dst, in0=src, scalar1=mean_vars[u][:, r, 0:1], scalar2=rstd[:, r : r + 1],
                     op0=ALU.subtract, op1=ALU.mult,
                 )
 
         h_plane = {}
 
-        def flip_tokens(u, g, vector_banks=0):
+        def flip_tokens(u, g):
             if g == 0:
                 h_plane[u] = planes.tile([P, CHUNKS, UNIT], BF16, name="h_plane", tag="h_plane")
             for b in range(PACK // PAIR):
@@ -268,27 +257,18 @@ def tile_siglipencoderlayer_pa_kernel(
                     gain = gain_bias[:, f : f + 1]
                     bias = gain_bias[:, CHUNKS + f : CHUNKS + f + 1]
                     src = bank[:, s * UNIT : (s + 1) * UNIT]
-                    if b < vector_banks:
-                        nc.vector.tensor_scalar(
-                            out=h_plane[u][:, f, :], in0=src, scalar1=gain, scalar2=bias,
-                            op0=ALU.mult, op1=ALU.add,
-                        )
-                    else:
-                        nc.scalar.activation(
-                            out=h_plane[u][:, f, :], in_=src, func=ACT.Identity, scale=gain, bias=bias
-                        )
+                    nc.scalar.activation(
+                        out=h_plane[u][:, f, :], in_=src, func=ACT.Identity, scale=gain, bias=bias
+                    )
 
         h_grouped = {}
 
-        def group_tokens(u, g, engine="vector"):
+        def group_tokens(u, g):
             if g == 0:
                 h_grouped[u] = grouped.tile([P, PASSES, UNIT * PACK], BF16, name="h_grouped", tag="h_grouped", align_bytes=64)
-            dst = h_grouped[u][:, g, :].rearrange("p (c i t) -> p c t i", i=PACK, t=PACK)
-            src = h_plane[u][:, g * PACK : (g + 1) * PACK, :].rearrange("p t (c i) -> p c t i", i=PACK)
-            if engine == "vector":
-                nc.vector.tensor_copy(out=dst, in_=src)
-            else:
-                nc.scalar.copy(out=dst, in_=src)
+            dst = h_grouped[u][:, g, :].rearrange("p (n t) -> p n t", t=PACK)
+            src = h_plane[u][:, g * PACK : (g + 1) * PACK, :].rearrange("p t n -> p n t")
+            nc.vector.tensor_copy(out=dst, in_=src)
 
         def pack_tokens(u):
             nc.vector.quantize_mx(
@@ -330,11 +310,11 @@ def tile_siglipencoderlayer_pa_kernel(
 
         accs = {}
 
-        def merged(n, h, nt, part):
-            if part == 0:
+        def merged(n, h, nt, part, tiles=range(PAIR)):
+            if part == 0 and 0 in tiles:
                 accs[(n, h, nt)] = banks.tile([P, N_TILE], F32, name="acc", tag="bank")
             acc = accs[(n, h, nt)]
-            for r in range(PAIR):
+            for r in tiles:
                 for g in range(PASSES):
                     one_pass(
                         acc, n, h * MERGE + part * PAIR + r, g, nt,
@@ -372,135 +352,127 @@ def tile_siglipencoderlayer_pa_kernel(
                     out=merged_views[n][:, h, nt * N_TILE + s * half : nt * N_TILE + (s + 1) * half], in_=rows[:]
                 )
 
+        def flip_tile(n, nt):
+            for i in range(RUN):
+                flip_weight(n, nt, i)
 
-        def weights_run(first, last):
-            for c in range(first, last):
-                flip_weight(*blocks[c])
+        def sort_tile(n, nt):
+            for i in range(RUN):
+                sort_weight(n, nt, i)
 
-        def stats(u):
-            join_moments(2 * u)
-            join_moments(2 * u + 1)
-            finish_measure(u)
+        def join(u):
+            for r in range(PAIR):
+                join_moments(PAIR * u + r)
 
-        def tokens(u):
-            flip_tokens(u, 0)
-            flip_tokens(u, 1)
+        def normalise_unit(u):
+            for r in range(PAIR):
+                normalise(PAIR * u + r)
 
-        def pack(u):
-            group_tokens(u, 0)
-            group_tokens(u, 1)
-            pack_tokens(u)
+        def flip_unit(u):
+            for g in range(PASSES):
+                flip_tokens(u, g)
 
-        def sort_run(first, last, engine="scalar"):
-            for c in range(first, last):
-                sort_weight(*blocks[c], engine)
+        def group_unit(u):
+            for g in range(PASSES):
+                group_tokens(u, g)
+
+        def queries_of(nt, *units):
+            for u in units:
+                for r in range(PAIR):
+                    queries(PAIR * u + r, nt)
 
         measure_tile(0)
-        weights_run(0, 1)
-        measure_tile(1)
+        measure_tile(1, [0])
         join_moments(0)
+        invert_std(0, 0, 1)
+        flip_weight("k", 0, 0)
+        measure_tile(1, [1])
         join_moments(1)
-        finish_measure(0)
-        weights_run(1, 4)
-        normalise(0)
-        normalise(1)
+        invert_std(0, 1, 1)
+        for i in range(1, RUN):
+            flip_weight("k", 0, i)
+        normalise_unit(0)
         flip_gain_bias()
-        tokens(0)
+        flip_unit(0)
         measure_tile(2)
         measure_tile(3)
+
         pack_weight("k", 0)
-        join_moments(2)
-        join_moments(3)
-        weights_run(4, 7)
-        group_tokens(0, 0)
-        group_tokens(0, 1)
-        finish_measure(1)
+        join(1)
+        for i in range(RUN - 1):
+            flip_weight("k", 1, i)
+        group_unit(0)
+        invert_std(1)
+        flip_weight("k", 1, RUN - 1)
         measure_tile(4)
-        finish_shift(1)
-        weights_run(7, 10)
+        find_shift(1)
         pack_tokens(0)
+        flip_tile("v", 0)
         measure_tile(5)
-        weights_run(10, 12)
-        join_moments(4)
         normalise(3, "scalar")
         normalise(2)
-        join_moments(5)
-        weights_run(12, 14)
-        merged("k", 0, 0, 0)
-        finish_measure(2)
+        join(2)
+        flip_weight("v", 1, 0)
+        merged("k", 0, 0, 0, [0])
+        flip_weight("v", 1, 1)
+        merged("k", 0, 0, 0, [1])
+        invert_std(2)
+        flip_unit(1)
+
         pack_weight("v", 0)
-        tokens(1)
-        sort_run(16, 17)
         pack_weight("k", 1)
-        normalise(4)
-        normalise(5)
-        group_tokens(1, 0)
-        group_tokens(1, 1)
-        weights_run(14, 16)
-        sort_run(17, 19)
+        normalise_unit(2)
+        flip_weight("v", 1, 2)
+        flip_weight("v", 1, 3)
+        group_unit(1)
+        sort_tile("q", 0)
         merged("k", 0, 1, 0)
         merged("v", 0, 0, 0)
         measure_tile(6)
         pack_tokens(1)
         measure_tile(7)
-        join_moments(6)
-        join_moments(7)
-        sort_run(19, 20)
-        finish_measure(3)
-        weights_run(16, 17)
-        tokens(2)
+        join(3)
+        sort_weight("q", 1, 0)
+        invert_std(3)
+        flip_unit(2)
+
+        sort_weight("q", 1, 1)
         pack_weight("v", 1)
-        normalise(6)
-        normalise(7)
+        normalise_unit(3)
         merged("k", 0, 0, 1)
         merged("k", 0, 1, 1)
         merged("v", 0, 0, 1)
         settle("k", 0, 0)
-        group_tokens(2, 0)
-        group_tokens(2, 1)
-        weights_run(17, 20)
-        sort_run(20, 21)
+        group_unit(2)
+        flip_tile("q", 0)
         pack_tokens(2)
         settle("k", 0, 1)
         merged("v", 0, 1, 0)
         merged("v", 0, 1, 1)
-        tokens(3)
-        sort_run(21, 24)
+        sort_weight("q", 1, 2)
+        flip_unit(3)
+        sort_weight("q", 1, 3)
+
         pack_weight("q", 0)
-        merged("k", 1, 0, 0)
         settle("v", 0, 0)
         settle("v", 0, 1)
-        group_tokens(3, 0)
-        group_tokens(3, 1)
-        parts = [(n, nt, part) for n in "kv" for nt in range(N_TILES) for part in range(2)]
-        def tail_part(j):
-            n, nt, part = parts[j]
-            merged(n, 1, nt, part)
-            if part == 1:
-                settle(n, 1, nt)
-
-        queries(0, 0)
-        queries(1, 0)
-        queries(2, 0)
-        weights_run(20, 24)
+        group_unit(3)
+        merged("k", 1, 0, 0)
+        merged("k", 1, 1, 0)
+        queries_of(0, 0)
+        flip_tile("q", 1)
         pack_tokens(3)
-        queries(3, 0)
-        queries(4, 0)
-        queries(5, 0)
+        queries_of(0, 1, 2)
         pack_weight("q", 1)
-        tail_part(1)
-        tail_part(2)
-        queries(6, 0)
-        queries(7, 0)
-        tail_part(3)
-        queries(0, 1)
-        queries(1, 1)
-        tail_part(4)
-        queries(2, 1)
-        queries(3, 1)
-        queries(4, 1)
-        queries(5, 1)
-        tail_part(5)
-        queries(6, 1)
-        queries(7, 1)
+
+        merged("k", 1, 0, 1)
+        settle("k", 1, 0)
+        queries_of(0, 3)
+        merged("k", 1, 1, 1)
+        settle("k", 1, 1)
+        queries_of(1, 0, 1)
+        merged("v", 1, 0, 0)
+        merged("v", 1, 0, 1)
+        settle("v", 1, 0)
+        queries_of(1, 2, 3)
         last_products(1)

from contextlib import ExitStack

import concourse.mybir as mybir
from concourse.masks import make_identity

F32 = mybir.dt.float32
BF16 = mybir.dt.bfloat16
U32 = mybir.dt.uint32
U8 = mybir.dt.uint8
FP8X4 = mybir.dt.float8_e4m3fn_x4
ACT = mybir.ActivationFunctionType
ALU = mybir.AluOpType

P = 128
TOKENS = 1024
D = 1024
E = 1024
MERGE = 4
EPS = 1e-6
PACK = 4
K_PASS = P * PACK
PASSES = D // K_PASS
CHUNKS = D // P
HALF = P * MERGE
HALVES = TOKENS // HALF
TILES = TOKENS // P
PAIR = 2
UNITS = TILES // PAIR
UNIT = PAIR * P
N_TILE = 512
N_TILES = E // N_TILE
RUN = N_TILE // P
BN_MAX = 512

LAST = ("v", 1)

FLOPS = 2 * 3 * TOKENS * D * E


def tile_siglipencoderlayer_pa_kernel(
    tc, x, ln1_g, ln1_b, Wq, bq, Wk, bk, Wv, bv, out_0, out_1, out_2
):
    nc = tc.nc
    x_view = x.flatten_outer_dims().rearrange("(h j r) d -> j h (r d)", h=HALVES, r=MERGE)
    q_view = out_0.flatten_outer_dims().rearrange("(h j r) e -> j h r e", h=HALVES, r=MERGE)
    merged_views = {
        "k": out_1.flatten_outer_dims().rearrange("(h j) e -> j h e", h=HALVES),
        "v": out_2.flatten_outer_dims().rearrange("(h j) e -> j h e", h=HALVES),
    }
    weights = {"q": Wq, "k": Wk, "v": Wv}
    biases = {"q": bq, "k": bk, "v": bv}

    with ExitStack() as stack:
        consts = stack.enter_context(tc.tile_pool(name="consts", bufs=1))
        raw = stack.enter_context(tc.tile_pool(name="raw", bufs=1))
        small = stack.enter_context(tc.tile_pool(name="small", bufs=4))
        normed = stack.enter_context(tc.tile_pool(name="normed", bufs=6))
        planes = stack.enter_context(tc.tile_pool(name="planes", bufs=2))
        grouped = stack.enter_context(tc.tile_pool(name="grouped", bufs=4))
        sortp = stack.enter_context(tc.tile_pool(name="sortp", bufs=2 * RUN))
        packed = stack.enter_context(tc.tile_pool(name="packed", bufs=1))
        results = stack.enter_context(tc.tile_pool(name="results", bufs=10))
        banks = stack.enter_context(tc.psum_pool(name="banks", bufs=8))
        stack.enter_context(tc.manual_schedule())

        ident = consts.tile([P, P], F32, name="ident")
        make_identity(nc, ident[:])
        gb_rows = consts.tile([P, K_PASS], BF16, name="gb_rows")
        nc.vector.memset(gb_rows[:], 0.0)
        nc.scalar.dma_start(out=gb_rows[0:PASSES, :], in_=ln1_g.rearrange("(c w) -> c w", c=PASSES))
        nc.scalar.dma_start(out=gb_rows[PASSES : 2 * PASSES, :], in_=ln1_b.rearrange("(c w) -> c w", c=PASSES))
        eps = consts.tile([P, 1], F32, name="eps")
        nc.vector.memset(eps[:], EPS)
        warm = consts.tile([P, 1], F32, name="warm")
        nc.scalar.activation(out=warm[:], in_=eps[:], func=ACT.Abs_reciprocal_sqrt)


        x_raw = [raw.tile([P, PAIR * D], BF16, name="x_raw%d" % u) for u in range(UNITS)]
        w_raw = {n: raw.tile([P, N_TILES, RUN * D], BF16, name="w_raw_" + n) for n in "qkv"}
        bias_all = {n: consts.tile([P, E], BF16, name="bias_all_" + n) for n in "qkv"}

        def load_tokens(u, first, count):
            src = slice((u % (UNITS // HALVES) * PAIR + first) * D, (u % (UNITS // HALVES) * PAIR + first + count) * D)
            nc.sync.dma_start(
                out=x_raw[u][:, first * D : (first + count) * D], in_=x_view[:, u // (UNITS // HALVES), src]
            )

        def load_weights(n, nt, first, count):
            rows = weights[n].rearrange("(nt p i) d -> p nt (i d)", nt=N_TILES, i=RUN)
            cols = slice(first * D, (first + count) * D)
            nc.sync.dma_start(out=w_raw[n][:, nt, cols], in_=rows[:, nt, cols])

        def load_bias(n):
            nc.sync.dma_start(out=bias_all[n][:], in_=biases[n].partition_broadcast(P))

        load_tokens(0, 0, 1)
        load_tokens(0, 1, 1)
        for i in range(RUN):
            load_weights("k", 0, i, 1)
        load_tokens(1, 0, PAIR)
        load_weights("k", 1, 0, 2)
        load_weights("k", 1, 2, 2)
        load_weights("v", 0, 0, 2)
        load_tokens(2, 0, PAIR)
        load_weights("v", 0, 2, 2)
        load_weights("v", 1, 0, 2)
        load_tokens(3, 0, PAIR)
        load_weights("v", 1, 2, 2)
        load_weights("q", 0, 0, RUN)
        load_weights("q", 1, 0, RUN)
        for n in "kvq":
            load_bias(n)

        gain_bias = consts.tile([P, 2 * CHUNKS], F32, name="gain_bias")
        h_words = packed.tile([P, UNITS, PASSES * UNIT], U32, name="h_words", align_bytes=64)
        h_scales = packed.tile([P, UNITS, PASSES * UNIT], U8, name="h_scales", align_bytes=64)
        w_words = {
            n: packed.tile([P, N_TILES, PASSES * N_TILE], U32, name="w_words_" + n, align_bytes=64)
            for n in "qkv"
        }
        w_scales = {
            n: packed.tile([P, N_TILES, PASSES * N_TILE], U8, name="w_scales_" + n, align_bytes=64)
            for n in "qkv"
        }
        w_grouped = {}
        xn_tiles = {}
        rstds = {}
        shifts = {}
        mean_vars = {}

        def flip_gain_bias():
            bank = banks.tile([P, N_TILE], F32, tag="bank")
            words = gb_rows[:].bitcast(F32).rearrange("p (q u) -> p u q", u=2)
            for u in range(2):
                nc.tensor.transpose(out=bank[:, u * P : (u + 1) * P], in_=words[:, u, :], identity=ident[:])
            src = bank[:].bitcast(BF16)[:, 0 : 4 * P].rearrange("p (u c e) -> p c u e", u=2, e=2)
            nc.scalar.copy(
                out=gain_bias[:].rearrange("p (c u e) -> p c u e", u=2, e=2), in_=src[:, 0 : 2 * PASSES, :, :]
            )

        def parts_of(n, nt):
            return 2 if (n, nt) == LAST else 1

        sorted_words = {}

        def sort_weight(n, nt, i):
            tile_ = sortp.tile([P, RUN * P], F32, tag="sorted")
            sorted_words[(n, nt, i)] = tile_
            dst = tile_[:].rearrange("p (g u q) -> p g u q", g=PASSES, u=2)
            src = w_raw[n][:, nt, i * D : (i + 1) * D].bitcast(F32).rearrange(
                "p (g q u) -> p g u q", g=PASSES, u=2
            )
            nc.scalar.copy(out=dst, in_=src)

        def flip_weight(n, nt, i):
            if i == 0:
                w_grouped[(n, nt)] = grouped.tile(
                    [P, PASSES * N_TILE * PACK], BF16, name="w_grouped", tag="w_grouped", align_bytes=64
                )
            words_in = w_raw[n][:, nt, :].bitcast(F32).rearrange(
                "p (i g q u) -> p i g u q", i=RUN, g=PASSES, u=2
            )
            words_out = w_grouped[(n, nt)][:].bitcast(F32).rearrange(
                "p (g e u) -> p g e u", g=PASSES, u=2
            )
            bank = banks.tile([P, N_TILE], F32, tag="bank")
            for c in range(PASSES * 2):
                if (n, nt, i) in sorted_words:
                    src = sorted_words[(n, nt, i)][:, c * P : (c + 1) * P]
                else:
                    src = words_in[:, i, c // 2, c % 2, :]
                nc.tensor.transpose(out=bank[:, c * P : (c + 1) * P], in_=src, identity=ident[:])
            src = bank[:].rearrange("p (g u e) -> p g e u", g=PASSES, u=2)
            parts = parts_of(n, nt)
            width = P // parts
            for s in range(parts):
                first = (s * RUN + i) * width
                dst = words_out[:, :, first : first + width, :]
                part_src = src[:, :, s * width : (s + 1) * width, :]
                nc.scalar.copy(out=dst, in_=part_src)

        def pack_weight(n, nt):
            nc.vector.quantize_mx(
                out=w_words[n][:, nt, :].bitcast(FP8X4),
                scales=w_scales[n][:, nt, :],
                in_=w_grouped[(n, nt)][:],
            )

        stats_tiles = {}

        def measure_tile(i, halves=range(D // BN_MAX)):
            u, r = i // PAIR, i % PAIR
            if 0 in halves:
                stats_tiles[i] = small.tile([P, D // BN_MAX, 6], F32, name="stats", tag="stats")
            for s in halves:
                first = r * D + s * BN_MAX
                nc.vector.bn_stats(out=stats_tiles[i][:, s, :], in_=x_raw[u][:, first : first + BN_MAX])

        def join_moments(i):
            u = i // PAIR
            if i % PAIR == 0:
                mean_vars[u] = small.tile([P, PAIR, 2], F32, name="mean_var", tag="mean_var")
            nc.vector.bn_aggr(
                out=mean_vars[u][:, i % PAIR, :], in_=stats_tiles[i][:].rearrange("p s k -> p (s k)")
            )

        def invert_std(u, first=0, count=PAIR):
            if first == 0:
                rstds[u] = small.tile([P, PAIR], F32, name="rstd", tag="rstd")
            tiles = slice(first, first + count)
            nc.scalar.activation(
                out=rstds[u][:, tiles], in_=mean_vars[u][:, tiles, 1], func=ACT.Abs_reciprocal_sqrt, bias=eps[:, 0:1]
            )

        def find_shift(u):
            shift = small.tile([P, PAIR], F32, tag="shift")
            nc.vector.scalar_tensor_tensor(
                out=shift[:], in0=mean_vars[u][:, :, 0], scalar=-1.0, in1=rstds[u][:],
                op0=ALU.mult, op1=ALU.mult,
            )
            shifts[u] = shift

        def normalise(i, engine="vector"):
            u, r = i // PAIR, i % PAIR
            rstd = rstds[u]
            xn = normed.tile([P, D], F32, tag="xn")
            xn_tiles[i] = xn
            dst = xn[:].rearrange("p (g t q) -> p g q t", g=PASSES, t=PACK)
            src = x_raw[u][:, r * D : (r + 1) * D].rearrange("p (g q t) -> p g q t", g=PASSES, t=PACK)
            if engine == "scalar":
                nc.scalar.activation(
                    out=dst, in_=src, func=ACT.Identity, scale=rstd[:, r : r + 1], bias=shifts[u][:, r : r + 1]
                )
            else:
                nc.vector.tensor_scalar(
                    out=dst, in0=src, scalar1=mean_vars[u][:, r, 0:1], scalar2=rstd[:, r : r + 1],
                    op0=ALU.subtract, op1=ALU.mult,
                )

        h_plane = {}

        def flip_tokens(u, g):
            if g == 0:
                h_plane[u] = planes.tile([P, CHUNKS, UNIT], BF16, name="h_plane", tag="h_plane")
            for b in range(PACK // PAIR):
                bank = banks.tile([P, N_TILE], F32, tag="bank")
                for s in range(PAIR):
                    f = g * PACK + b * PAIR + s
                    for r in range(PAIR):
                        nc.tensor.transpose(
                            out=bank[:, s * UNIT + r * P : s * UNIT + (r + 1) * P],
                            in_=xn_tiles[u * PAIR + r][:, f * P : (f + 1) * P],
                            identity=ident[:],
                        )
                for s in range(PAIR):
                    f = g * PACK + b * PAIR + s
                    gain = gain_bias[:, f : f + 1]
                    bias = gain_bias[:, CHUNKS + f : CHUNKS + f + 1]
                    src = bank[:, s * UNIT : (s + 1) * UNIT]
                    nc.scalar.activation(
                        out=h_plane[u][:, f, :], in_=src, func=ACT.Identity, scale=gain, bias=bias
                    )

        h_grouped = {}

        def group_tokens(u, g):
            if g == 0:
                h_grouped[u] = grouped.tile([P, PASSES, UNIT * PACK], BF16, name="h_grouped", tag="h_grouped", align_bytes=64)
            dst = h_grouped[u][:, g, :].rearrange("p (n t) -> p n t", t=PACK)
            src = h_plane[u][:, g * PACK : (g + 1) * PACK, :].rearrange("p t n -> p n t")
            nc.vector.tensor_copy(out=dst, in_=src)

        def pack_tokens(u):
            nc.vector.quantize_mx(
                out=h_words[:, u, :].bitcast(FP8X4), scales=h_scales[:, u, :],
                in_=h_grouped[u][:].rearrange("p g w -> p (g w)"),
            )

        def one_pass(acc, n, i, g, nt, start, stop, first=0, width=N_TILE):
            u = i // PAIR
            toks = slice(g * UNIT + (i % PAIR) * P, g * UNIT + (i % PAIR) * P + P)
            cols = slice(g * N_TILE + first, g * N_TILE + first + width)
            nc.tensor.matmul_mx(
                out=acc[:, first : first + width],
                lhsT=h_words[:, u, toks].bitcast(FP8X4),
                lhsT_scale=h_scales[:, u, toks],
                rhs=w_words[n][:, nt, cols].bitcast(FP8X4),
                rhs_scale=w_scales[n][:, nt, cols],
                start=start,
                stop=stop,
            )

        def by_feature(acc, first=0, width=N_TILE):
            return acc[:, first : first + width].rearrange("q (i p) -> q p i", i=RUN)

        def natural(tile_, first, width=N_TILE):
            return tile_[:, first : first + width].rearrange("q (p i) -> q p i", i=RUN)

        def queries(i, nt):
            acc = banks.tile([P, N_TILE], F32, tag="bank")
            for g in range(PASSES):
                one_pass(acc, "q", i, g, nt, g == 0, g == PASSES - 1)
            rows = results.tile([P, N_TILE], F32, tag="rows")
            nc.vector.tensor_tensor(
                out=natural(rows, 0), in0=by_feature(acc), in1=natural(bias_all["q"], nt * N_TILE), op=ALU.add
            )
            nc.sync.dma_start(
                out=q_view[:, i // MERGE, i % MERGE, nt * N_TILE : (nt + 1) * N_TILE], in_=rows[:]
            )

        accs = {}

        def merged(n, h, nt, part, tiles=range(PAIR)):
            if part == 0 and 0 in tiles:
                accs[(n, h, nt)] = banks.tile([P, N_TILE], F32, name="acc", tag="bank")
            acc = accs[(n, h, nt)]
            for r in tiles:
                for g in range(PASSES):
                    one_pass(
                        acc, n, h * MERGE + part * PAIR + r, g, nt,
                        part == 0 and r == 0 and g == 0, part == 1 and r == PAIR - 1 and g == PASSES - 1,
                    )

        def settle(n, h, nt):
            width = N_TILE // parts_of(n, nt)
            rows = results.tile([P, N_TILE], F32, tag="rows")
            for first in range(0, N_TILE, width):
                nc.vector.scalar_tensor_tensor(
                    out=natural(rows, first, width), in0=by_feature(accs[(n, h, nt)], first, width),
                    scalar=1.0 / MERGE, in1=natural(bias_all[n], nt * N_TILE + first, width),
                    op0=ALU.mult, op1=ALU.add,
                )
            nc.sync.dma_start(out=merged_views[n][:, h, nt * N_TILE : (nt + 1) * N_TILE], in_=rows[:])

        def last_products(h):
            n, nt = LAST
            half = N_TILE // 2
            for s in range(2):
                acc = banks.tile([P, N_TILE], F32, name="acc", tag="bank")
                for i in range(h * MERGE, (h + 1) * MERGE):
                    for g in range(PASSES):
                        one_pass(
                            acc, n, i, g, nt, i == h * MERGE and g == 0,
                            i == (h + 1) * MERGE - 1 and g == PASSES - 1, s * half, half,
                        )
                rows = results.tile([P, half], F32, name="half_rows", tag="half_rows")
                nc.vector.scalar_tensor_tensor(
                    out=natural(rows, 0, half), in0=by_feature(acc, s * half, half), scalar=1.0 / MERGE,
                    in1=natural(bias_all[n], nt * N_TILE + s * half, half), op0=ALU.mult, op1=ALU.add,
                )
                nc.sync.dma_start(
                    out=merged_views[n][:, h, nt * N_TILE + s * half : nt * N_TILE + (s + 1) * half], in_=rows[:]
                )

        def flip_tile(n, nt):
            for i in range(RUN):
                flip_weight(n, nt, i)

        def sort_tile(n, nt):
            for i in range(RUN):
                sort_weight(n, nt, i)

        def join(u):
            for r in range(PAIR):
                join_moments(PAIR * u + r)

        def normalise_unit(u):
            for r in range(PAIR):
                normalise(PAIR * u + r)

        def flip_unit(u):
            for g in range(PASSES):
                flip_tokens(u, g)

        def group_unit(u):
            for g in range(PASSES):
                group_tokens(u, g)

        def queries_of(nt, *units):
            for u in units:
                for r in range(PAIR):
                    queries(PAIR * u + r, nt)

        measure_tile(0)
        measure_tile(1, [0])
        join_moments(0)
        invert_std(0, 0, 1)
        flip_weight("k", 0, 0)
        measure_tile(1, [1])
        join_moments(1)
        invert_std(0, 1, 1)
        for i in range(1, RUN):
            flip_weight("k", 0, i)
        normalise_unit(0)
        flip_gain_bias()
        flip_unit(0)
        measure_tile(2)
        measure_tile(3)

        pack_weight("k", 0)
        join(1)
        for i in range(RUN - 1):
            flip_weight("k", 1, i)
        group_unit(0)
        invert_std(1)
        flip_weight("k", 1, RUN - 1)
        measure_tile(4)
        find_shift(1)
        pack_tokens(0)
        flip_tile("v", 0)
        measure_tile(5)
        normalise(3, "scalar")
        normalise(2)
        join(2)
        flip_weight("v", 1, 0)
        merged("k", 0, 0, 0, [0])
        flip_weight("v", 1, 1)
        merged("k", 0, 0, 0, [1])
        invert_std(2)
        flip_unit(1)

        pack_weight("v", 0)
        pack_weight("k", 1)
        normalise_unit(2)
        flip_weight("v", 1, 2)
        flip_weight("v", 1, 3)
        group_unit(1)
        sort_tile("q", 0)
        merged("k", 0, 1, 0)
        merged("v", 0, 0, 0)
        measure_tile(6)
        pack_tokens(1)
        measure_tile(7)
        join(3)
        sort_weight("q", 1, 0)
        invert_std(3)
        flip_unit(2)

        sort_weight("q", 1, 1)
        pack_weight("v", 1)
        normalise_unit(3)
        merged("k", 0, 0, 1)
        merged("k", 0, 1, 1)
        merged("v", 0, 0, 1)
        settle("k", 0, 0)
        group_unit(2)
        flip_tile("q", 0)
        pack_tokens(2)
        settle("k", 0, 1)
        merged("v", 0, 1, 0)
        merged("v", 0, 1, 1)
        sort_weight("q", 1, 2)
        flip_unit(3)
        sort_weight("q", 1, 3)

        pack_weight("q", 0)
        settle("v", 0, 0)
        settle("v", 0, 1)
        group_unit(3)
        merged("k", 1, 0, 0)
        merged("k", 1, 1, 0)
        queries_of(0, 0)
        flip_tile("q", 1)
        pack_tokens(3)
        queries_of(0, 1, 2)
        pack_weight("q", 1)

        merged("k", 1, 0, 1)
        settle("k", 1, 0)
        queries_of(0, 3)
        merged("k", 1, 1, 1)
        settle("k", 1, 1)
        queries_of(1, 0, 1)
        merged("v", 1, 0, 0)
        merged("v", 1, 0, 1)
        settle("v", 1, 0)
        queries_of(1, 2, 3)
        last_products(1)
